import numpy as np
import ml_dtypes


def mxq(x, axis, fmt="e4m3"):
    dtype, down = {"e4m3": (ml_dtypes.float8_e4m3fn, 7), "e5m2": (ml_dtypes.float8_e5m2, 14)}[fmt]
    v = np.moveaxis(np.asarray(x, np.float32).astype(ml_dtypes.bfloat16).astype(np.float64), axis, -1)
    blocks = v.reshape(v.shape[:-1] + (-1, 32))
    amax = np.abs(blocks).max(-1, keepdims=True)
    byte = np.maximum(np.where(amax > 0, np.frexp(amax)[1] - 1 + 127, 0) - down, 1)
    scale = np.exp2(byte - 127.0)
    codes = (blocks / scale).astype(np.float32).astype(dtype).astype(np.float64)
    return np.moveaxis((codes * scale).reshape(v.shape), -1, axis)


WIDE = False


def mx_kscale(k):
    if not WIDE:
        return np.ones(k)
    levels = np.array([10, -10, 5, -5, 0])
    a = np.random.permutation(np.resize(levels, k // 512 * 4)).reshape(k // 512, 4)
    idx = np.arange(k)
    return np.exp2(a[idx // 512, idx % 128 // 32])


BF16 = ml_dtypes.bfloat16


def bf(x):
    return np.asarray(x, np.float32).astype(BF16)


def f64(x):
    return np.asarray(x).astype(np.float64)


B, N, D, H, HD, S, DO = 2, 4096, 1024, 2, 64, 11, 1024
E = H * HD
D4 = [0.4829629131445341, 0.8365163037378079, 0.2241438680420134, -0.1294095225512604]
T = len(D4)


def elu1(u):
    return np.where(u > 0.0, u, np.exp(np.minimum(u, 0.0)) - 1.0) + 1.0


def softplus(u):
    return np.log(1.0 + np.exp(u))


def shifted(t, o):
    if o == 0:
        return t
    return np.concatenate([np.zeros((B, H, o, HD)), t[:, :, :N - o, :]], axis=2)


def setup_inputs():
    s = mx_kscale(D)
    lg = np.random.standard_normal((B, H, N, S)) * 1.4
    g = np.exp(lg - lg.max(-1, keepdims=True))
    return {"x": bf(np.random.standard_normal((B, N, D)) * s),
            "W_qkv": bf(np.random.standard_normal((3 * E, D)) * 0.6 / np.sqrt(D) / s),
            "b_qkv": bf(np.random.standard_normal(3 * E) * 0.1),
            "gains": bf(g / g.sum(-1, keepdims=True)),
            "pos_bias": bf(np.random.standard_normal((S * T, H)) * 0.5),
            "identity_bypass": bf(-1.0 + 0.5 * np.random.standard_normal(H))}


def reference(x, W_qkv, b_qkv, gains, pos_bias, identity_bypass):
    qkv = (mxq(f64(x), 2, "e4m3") @ mxq(f64(W_qkv), 1, "e4m3").T) + f64(b_qkv)
    q, k, v = [t.reshape(B, N, H, HD).transpose(0, 2, 1, 3) for t in np.split(qkv, 3, axis=-1)]
    g, pb = f64(gains), f64(pos_bias)
    acc = np.zeros((B, H, N, HD))
    z = np.zeros((B, H, N, 1))
    tap = 0
    for j in range(S):
        d = 1 << j
        g_j = g[..., j][..., None]
        for tau, c in enumerate(D4):
            o = d * tau
            bias = pb[tap].reshape(1, H, 1, 1)
            tap += 1
            if o != 0 and o >= N:
                continue
            k_s, v_s = shifted(k, o), shifted(v, o)
            feat = elu1(np.sum(q * k_s, -1, keepdims=True) + bias)
            acc = acc + (g_j * c) * feat * v_s
            z = z + g_j * abs(c) * feat
    p = softplus(f64(identity_bypass)).reshape(1, H, 1, 1)
    local = elu1(np.sum(q * k, -1, keepdims=True))
    acc = acc + p * local * v
    z = z + p * local
    res = acc / (z + 1e-06)
    return res.transpose(0, 2, 1, 3).reshape(B, N, E)

@@ -1,0 +1,401 @@
+from contextlib import ExitStack
+
+import concourse.mybir as mybir
+from concourse.masks import make_identity
+
+F32 = mybir.dt.float32
+BF16 = mybir.dt.bfloat16
+U32 = mybir.dt.uint32
+U8 = mybir.dt.uint8
+FP8X4 = mybir.dt.float8_e4m3fn_x4
+ALU = mybir.AluOpType
+ACTF = mybir.ActivationFunctionType
+AX = mybir.AxisListType
+
+P = 128
+B, N, D, H, HD, NS = 2, 4096, 1024, 2, 64, 11
+E = H * HD
+CH = 512
+TPC = CH // P
+NCC = N // CH
+NT = N // P
+NCHUNK = B * NCC
+WIN = 256
+D4 = (0.4829629131445341, 0.8365163037378079, 0.2241438680420134, -0.1294095225512604)
+OFFS = tuple(sorted([0] + [1 << i for i in range(12)] + [3 << j for j in range(11)]))
+NOFF = 24
+NTAP = 45
+FLOPS = 2 * B * N * D * 3 * E + 4 * B * H * N * HD * NOFF
+ACT_SHARE = (0, 2, 4, 6)
+PINNED = False
+
+
+def n_valid(t):
+    return len([o for o in OFFS if o <= t * P + P - 1])
+
+
+def runs_of(slots):
+    runs = []
+    for place, slot in slots:
+        if runs and runs[-1][0] + runs[-1][2] == place and runs[-1][1] + runs[-1][2] == slot:
+            runs[-1][2] += 1
+        else:
+            runs.append([place, slot, 1])
+    return runs
+
+
+def tile_dwarfattention_pa_t_kernel(tc, x, W_qkv, b_qkv, gains, pos_bias, identity_bypass, out):
+    nc = tc.nc
+    with ExitStack() as ctx:
+        const = ctx.enter_context(tc.tile_pool(name="const", bufs=1))
+        ps_xt = ctx.enter_context(tc.psum_pool(name="ps_xt", bufs=2))
+        ps_mm = ctx.enter_context(tc.psum_pool(name="ps_mm", bufs=2))
+        ps_ko = ctx.enter_context(tc.psum_pool(name="ps_ko", bufs=4))
+
+        ident = const.tile([P, P], F32, name="ident")
+        make_identity(nc, ident[:])
+
+        wc = const.tile([P, 2, 3 * P], U32, name="wc", align_bytes=64)
+        ws = const.tile([P, 2, 3 * P], U8, name="ws", align_bytes=64)
+        bias_col = const.tile([P, 4], F32, name="bias_col")
+        bq_bc = const.tile([P, E], F32, name="bq_bc")
+        pb_bc = const.tile([P, H, NTAP], F32, name="pb_bc")
+        gc = const.tile([P, B, H, NT, NTAP], F32, name="gc")
+        k_a = const.tile([P, B * NT, E], F32, name="k_a")
+        v_a = const.tile([P, B * NT, E], F32, name="v_a")
+        junk = const.tile([P, HD], F32, name="junk")
+
+        with tc.tile_pool(name="setup", bufs=1) as setup:
+            w_sb = setup.tile([P, 3, D], BF16, name="w_sb")
+            nc.sync.dma_start(out=w_sb[:], in_=W_qkv.rearrange("(f p) k -> p f k", p=P))
+            b_rows = setup.tile([P, P], BF16, name="b_rows")
+            nc.vector.memset(b_rows[:], 0.0)
+            nc.scalar.dma_start(out=b_rows[0:3, :], in_=b_qkv.rearrange("(f c) -> f c", c=P))
+            bq_raw = setup.tile([P, E], BF16, name="bq_raw")
+            nc.scalar.dma_start(out=bq_raw[:], in_=b_qkv[0:E].partition_broadcast(P))
+            pb_raw = setup.tile([P, 4 * NS * H], BF16, name="pb_raw")
+            nc.scalar.dma_start(out=pb_raw[:], in_=pos_bias.rearrange("r h -> (r h)").partition_broadcast(P))
+            ib_raw = setup.tile([P, H], BF16, name="ib_raw")
+            nc.scalar.dma_start(out=ib_raw[:], in_=identity_bypass.partition_broadcast(P))
+            g_raw = setup.tile([P, B, H, NT, NS], BF16, name="g_raw")
+            for b in range(B):
+                for h in range(H):
+                    nc.scalar.dma_start(out=g_raw[:, b, h, :, :], in_=gains[b, h].rearrange("(t p) j -> p t j", p=P))
+
+            wg = setup.tile([P, 2, 3 * P, 2], F32, name="wg", align_bytes=64)
+            for f in range(3):
+                wt = ps_xt.tile([P, 4, P], F32, name="wt", tag="xt")
+                ww = w_sb[:, f, :].bitcast(F32)
+                for j in range(4):
+                    nc.tensor.transpose(out=wt[:, j, :], in_=ww[:, j * P:(j + 1) * P], identity=ident[:])
+                nc.vector.tensor_copy(out=wg[:, :, f * P:(f + 1) * P, :],
+                                      in_=wt[:].rearrange("p (g u) r -> p g r u", u=2))
+            for g in range(2):
+                for f in range(3):
+                    nc.vector.quantize_mx(
+                        out=wc[:, g, f * P:(f + 1) * P].bitcast(FP8X4),
+                        scales=ws[:, g, f * P:(f + 1) * P],
+                        in_=wg[:, g, f * P:(f + 1) * P, :].rearrange("p r u -> p (r u)").bitcast(BF16))
+
+            b_rows32 = setup.tile([P, P], F32, name="b_rows32")
+            nc.vector.tensor_copy(out=b_rows32[:], in_=b_rows[:])
+            bt = ps_xt.tile([P, 4, P], F32, name="bt", tag="xt")
+            nc.tensor.transpose(out=bt[:, 0, :], in_=b_rows32[:], identity=ident[:])
+            nc.vector.tensor_copy(out=bias_col[:, 0:3], in_=bt[:, 0, 0:3])
+            nc.vector.tensor_copy(out=bq_bc[:], in_=bq_raw[:])
+
+            nc.vector.memset(pb_bc[:], 0.0)
+            nc.vector.tensor_copy(out=pb_bc[:, :, 1:NTAP].rearrange("p h (t j) -> p h t j", t=4),
+                                  in_=pb_raw[:].rearrange("p (j t h) -> p h t j", t=4, h=H))
+
+            ib = setup.tile([P, H], F32, name="ib")
+            nc.vector.tensor_copy(out=ib[:], in_=ib_raw[:])
+            ib_e = setup.tile([P, H], F32, name="ib_e")
+            nc.scalar.activation(out=ib_e[:], in_=ib[:], func=ACTF.Abs)
+            nc.scalar.activation(out=ib_e[:], in_=ib_e[:], func=ACTF.Exp, scale=-1.0)
+            nc.vector.tensor_scalar_add(out=ib_e[:], in0=ib_e[:], scalar1=1.0)
+            nc.scalar.activation(out=ib_e[:], in_=ib_e[:], func=ACTF.Ln)
+            sp = setup.tile([P, H], F32, name="sp")
+            nc.vector.scalar_tensor_tensor(out=sp[:], in0=ib[:], scalar=0.0, in1=ib_e[:], op0=ALU.max, op1=ALU.add)
+
+            gcv = gc[:].rearrange("p b h t k -> p (b h t) k")
+            grv = g_raw[:].rearrange("p b h t j -> p (b h t) j")
+            for tau in range(4):
+                nc.gpsimd.tensor_scalar(out=gcv[:, :, 1 + NS * tau:1 + NS * (tau + 1)], in0=grv,
+                                        scalar1=D4[tau], scalar2=0.0, op0=ALU.mult, op1=ALU.add)
+            for b in range(B):
+                for h in range(H):
+                    nc.gpsimd.tensor_copy(out=gc[:, b, h, :, 0:1],
+                                          in_=sp[:, h:h + 1].unsqueeze(1).to_broadcast([P, NT, 1]))
+
+        xp = ctx.enter_context(tc.tile_pool(name="xp", bufs=2))
+        gp = ctx.enter_context(tc.tile_pool(name="gp", bufs=2))
+        cp = ctx.enter_context(tc.tile_pool(name="cp", bufs=2))
+        kwp = ctx.enter_context(tc.tile_pool(name="kwp", bufs=3))
+        vwp = ctx.enter_context(tc.tile_pool(name="vwp", bufs=5))
+        qp = ctx.enter_context(tc.tile_pool(name="qp", bufs=3))
+        pp = ctx.enter_context(tc.tile_pool(name="pp", bufs=3))
+        sp_pool = ctx.enter_context(tc.tile_pool(name="sp_pool", bufs=3))
+        cm = ctx.enter_context(tc.tile_pool(name="cm", bufs=3))
+        accp = ctx.enter_context(tc.tile_pool(name="accp", bufs=2))
+
+        kw = {}
+        vw = {}
+        q_of = {}
+        s_of = {}
+
+        def window(c):
+            if c not in kw:
+                kw[c] = kwp.tile([P, WIN + CH], F32, name="kw")
+                vw[c] = vwp.tile([P, WIN + CH], F32, name="vw")
+            return kw[c], vw[c]
+
+        x_of = {}
+        grp_of = {}
+        code_of = {}
+
+        def fe_load(c):
+            b, cc = divmod(c, NCC)
+            n0 = cc * CH
+            x_sb = xp.tile([P, TPC, D], BF16, name="x_sb")
+            nc.sync.dma_start(out=x_sb[:], in_=x[b, n0:n0 + CH, :].rearrange("(t p) k -> p t k", p=P))
+            x_of[c] = x_sb
+
+        def fe_xpose(c, tl):
+            if tl == 0:
+                grp_of[c] = gp.tile([P, 2, CH, 2], F32, name="grp", align_bytes=64)
+            grp = grp_of[c]
+            xt = ps_xt.tile([P, 4, P], F32, name="xt", tag="xt")
+            xw = x_of[c][:, tl, :].bitcast(F32)
+            for j in range(4):
+                nc.tensor.transpose(out=xt[:, j, :], in_=xw[:, j * P:(j + 1) * P], identity=ident[:])
+            nc.scalar.copy(out=grp[:, :, tl * P:(tl + 1) * P, :],
+                           in_=xt[:].rearrange("p (g u) r -> p g r u", u=2))
+
+        def fe_quant(c):
+            grp = grp_of[c]
+            codes = cp.tile([P, 2, CH], U32, name="codes", align_bytes=64)
+            scl = cp.tile([P, 2, CH], U8, name="scl", align_bytes=64)
+            for g in range(2):
+                nc.vector.quantize_mx(out=codes[:, g, :].bitcast(FP8X4), scales=scl[:, g, :],
+                                      in_=grp[:, g, :, :].rearrange("p r u -> p (r u)").bitcast(BF16))
+            code_of[c] = (codes, scl)
+
+        def fe_kv(c):
+            b, cc = divmod(c, NCC)
+            codes, scl = code_of[c]
+            kwc, vwc = window(c)
+            if cc == 0:
+                nc.gpsimd.memset(kwc[:, 0:WIN], 0.0)
+                nc.gpsimd.memset(vwc[:, 0:WIN], 0.0)
+            for f, dst in ((1, kwc), (2, vwc)):
+                ps = ps_mm.tile([P, CH], F32, name="ps", tag="mm")
+                for g in range(2):
+                    nc.tensor.matmul_mx(out=ps[:], lhsT=wc[:, g, f * P:(f + 1) * P].bitcast(FP8X4),
+                                        lhsT_scale=ws[:, g, f * P:(f + 1) * P],
+                                        rhs=codes[:, g, :].bitcast(FP8X4), rhs_scale=scl[:, g, :],
+                                        start=(g == 0), stop=(g == 1))
+                nc.scalar.activation(out=dst[:, WIN:WIN + CH], in_=ps[:], func=ACTF.Identity,
+                                     bias=bias_col[:, f:f + 1], scale=1.0)
+                if cc + 1 < NCC:
+                    nxt = window(c + 1)[f - 1]
+                    nc.scalar.activation(out=nxt[:, 0:WIN], in_=ps[:, CH - WIN:CH], func=ACTF.Identity,
+                                         bias=bias_col[:, f:f + 1], scale=1.0)
+
+        def fe_q(c):
+            codes, scl = code_of[c]
+            psq = ps_mm.tile([P, TPC, E], F32, name="psq", tag="mm")
+            for tl in range(TPC):
+                for g in range(2):
+                    nc.tensor.matmul_mx(out=psq[:, tl, :], lhsT=codes[:, g, tl * P:(tl + 1) * P].bitcast(FP8X4),
+                                        lhsT_scale=scl[:, g, tl * P:(tl + 1) * P],
+                                        rhs=wc[:, g, 0:P].bitcast(FP8X4), rhs_scale=ws[:, g, 0:P],
+                                        start=(g == 0), stop=(g == 1))
+            q_sb = qp.tile([P, TPC, E], F32, name="q_sb")
+            nc.vector.tensor_tensor(out=q_sb[:], in0=psq[:], in1=bq_bc[:].unsqueeze(1).to_broadcast([P, TPC, E]),
+                                    op=ALU.add)
+            q_of[c] = q_sb
+
+        def fe_ka(c):
+            b, cc = divmod(c, NCC)
+            for src, dst in ((kw[c], k_a), (vw[c], v_a)):
+                ta = ps_xt.tile([P, TPC, P], F32, name="ta", tag="xt")
+                for tl in range(TPC):
+                    nc.tensor.transpose(out=ta[:, tl, :], in_=src[:, WIN + tl * P:WIN + (tl + 1) * P],
+                                        identity=ident[:])
+                nc.scalar.copy(out=dst[:, b * NT + cc * TPC:b * NT + (cc + 1) * TPC, :], in_=ta[:])
+
+        def shifted_groups(nv):
+            una = [s for s in range(nv) if OFFS[s] % P != 0]
+            return [una[i:i + 4] for i in range(0, len(una), 4)]
+
+        def scores(c, tl):
+            b, cc = divmod(c, NCC)
+            kwc = kw[c]
+            q_sb = q_of[c]
+            if tl == 0:
+                s_of[c] = sp_pool.tile([P, H, TPC, NOFF], F32, name="s_t")
+                if n_valid(cc * TPC) < NOFF:
+                    nc.gpsimd.memset(s_of[c][:], 0.0)
+            s_t = s_of[c]
+            for t in (cc * TPC + tl,):
+                nv = n_valid(t)
+                prod = pp.tile([P, NOFF, E], F32, name="prod")
+                qb = q_sb[:, tl, :]
+                for grp_s in shifted_groups(nv):
+                    ko = ps_ko.tile([P, 4, P], F32, name="ko", tag="ko")
+                    for i, s in enumerate(grp_s):
+                        col = WIN + tl * P - OFFS[s]
+                        nc.tensor.transpose(out=ko[:, i, :], in_=kwc[:, col:col + P], identity=ident[:])
+                    for i0, s0, ln in runs_of(list(enumerate(grp_s))):
+                        nc.vector.tensor_tensor(out=prod[:, s0:s0 + ln, :], in0=ko[:, i0:i0 + ln, :],
+                                                in1=qb.unsqueeze(1).to_broadcast([P, ln, E]), op=ALU.mult)
+                for s in range(nv):
+                    if OFFS[s] % P == 0:
+                        nc.vector.tensor_tensor(out=prod[:, s, :], in0=k_a[:, b * NT + t - OFFS[s] // P, :],
+                                                in1=qb, op=ALU.mult)
+                if (c * TPC + tl) % 7 in ACT_SHARE:
+                    for s in range(nv):
+                        for h in range(H):
+                            nc.scalar.activation(out=junk[:], in_=prod[:, s, h * HD:(h + 1) * HD], func=ACTF.Copy,
+                                                 accum_out=s_t[:, h, tl, s:s + 1])
+                else:
+                    pv = prod[:, 0:nv, :].rearrange("p s (h d) -> p (s h) d", h=H)
+                    for w in (32, 16, 8, 4, 2):
+                        nc.gpsimd.tensor_tensor(out=pv[:, :, 0:w], in0=pv[:, :, 0:w], in1=pv[:, :, w:2 * w],
+                                                op=ALU.add)
+                    p4 = prod[:, 0:nv, :].rearrange("p s (h d) -> p s h d", h=H)
+                    nc.gpsimd.tensor_tensor(out=s_t[:, :, tl, 0:nv].rearrange("p h s -> p s h"),
+                                            in0=p4[:, :, :, 0], in1=p4[:, :, :, 1], op=ALU.add)
+
+        def weights(c):
+            b, cc = divmod(c, NCC)
+            s_t = s_of[c]
+            shp = [P, H, TPC, NTAP]
+            u = cm.tile(shp, F32, name="u")
+            spair = s_t[:, :, :, 2:NOFF].rearrange("p h t (i two) -> p h t i two", two=2)
+
+            def pbs(lo, hi):
+                return pb_bc[:, :, lo:hi].unsqueeze(2).to_broadcast([P, H, TPC, hi - lo])
+
+            nc.gpsimd.tensor_tensor(out=u[:, :, :, 0:12], in0=s_t[:, :, :, 0:1].to_broadcast([P, H, TPC, 12]),
+                                    in1=pbs(0, 12), op=ALU.add)
+            nc.gpsimd.tensor_tensor(out=u[:, :, :, 12:13], in0=s_t[:, :, :, 1:2], in1=pbs(12, 13), op=ALU.add)
+            nc.gpsimd.tensor_tensor(out=u[:, :, :, 13:23], in0=spair[:, :, :, 0:10, 0], in1=pbs(13, 23), op=ALU.add)
+            nc.gpsimd.tensor_tensor(out=u[:, :, :, 23:34], in0=spair[:, :, :, 0:11, 0], in1=pbs(23, 34), op=ALU.add)
+            nc.gpsimd.tensor_tensor(out=u[:, :, :, 34:45], in0=spair[:, :, :, 0:11, 1], in1=pbs(34, 45), op=ALU.add)
+            e = cm.tile(shp, F32, name="e")
+            nc.gpsimd.tensor_scalar(out=e[:], in0=u[:], scalar1=0.0, scalar2=0.0, op0=ALU.min, op1=ALU.add)
+            nc.scalar.activation(out=e[:], in_=e[:], func=ACTF.Exp)
+            nc.scalar.activation(out=u[:], in_=u[:], func=ACTF.Relu)
+            nc.gpsimd.tensor_tensor(out=e[:], in0=e[:], in1=u[:], op=ALU.add)
+            wt = cm.tile(shp, F32, name="wt")
+            nc.gpsimd.tensor_tensor(out=wt[:], in0=e[:], in1=gc[:, b, :, cc * TPC:(cc + 1) * TPC, :], op=ALU.mult)
+            z1 = cm.tile([P, H, TPC], F32, name="z1")
+            z3 = cm.tile([P, H, TPC], F32, name="z3")
+            nc.vector.tensor_reduce(out=z1[:], in_=wt[:], axis=AX.X, op=ALU.add)
+            nc.vector.tensor_reduce(out=z3[:], in_=wt[:, :, :, 34:45], axis=AX.X, op=ALU.add)
+            nc.vector.scalar_tensor_tensor(out=z1[:], in0=z3[:], scalar=-2.0, in1=z1[:], op0=ALU.mult, op1=ALU.add)
+            nc.vector.tensor_scalar_add(out=z1[:], in0=z1[:], scalar1=1e-6)
+            nc.vector.reciprocal(out=z3[:], in_=z1[:])
+            wn = cm.tile(shp, F32, name="wn")
+            nc.gpsimd.tensor_tensor(out=wn[:], in0=wt[:], in1=z3[:].unsqueeze(3).to_broadcast(shp), op=ALU.mult)
+            w0 = cm.tile([P, H, TPC], F32, name="w0")
+            nc.vector.tensor_reduce(out=w0[:], in_=wn[:, :, :, 0:12], axis=AX.X, op=ALU.add)
+            wp = cm.tile([P, H, TPC, 10], F32, name="wp")
+            nc.gpsimd.tensor_tensor(out=wp[:], in0=wn[:, :, :, 13:23], in1=wn[:, :, :, 23:33], op=ALU.add)
+
+            def col(s, h, tl):
+                if s == 0:
+                    return w0[:, h, tl:tl + 1]
+                if s == 1:
+                    return wn[:, h, tl, 12:13]
+                if s % 2 == 0:
+                    i = s // 2
+                    if i <= 10:
+                        return wp[:, h, tl, i - 1:i]
+                    return wn[:, h, tl, 33:34]
+                j = (s - 3) // 2
+                return wn[:, h, tl, 34 + j:35 + j]
+
+            return col
+
+        acc_of = {}
+        col_of = {}
+
+        def values(c, pair):
+            b, cc = divmod(c, NCC)
+            vwc = vw[c]
+            col = col_of[c]
+            if pair == 0:
+                acc_of[c] = accp.tile([P, TPC, E], F32, name="acc")
+            acc = acc_of[c]
+
+            def mac(tl, s, src):
+                for h in range(H):
+                    hs = slice(h * HD, (h + 1) * HD)
+                    if s == 0:
+                        nc.vector.tensor_scalar_mul(out=acc[:, tl, hs], in0=src[:, hs], scalar1=col(s, h, tl))
+                    else:
+                        nc.vector.scalar_tensor_tensor(out=acc[:, tl, hs], in0=src[:, hs], scalar=col(s, h, tl),
+                                                       in1=acc[:, tl, hs], op0=ALU.mult, op1=ALU.add)
+
+            for tls in ((2 * pair, 2 * pair + 1),):
+                nvs = [n_valid(cc * TPC + tl) for tl in tls]
+                for k in range(NOFF):
+                    for tl, nv in zip(tls, nvs):
+                        if k < nv and OFFS[k] % P == 0:
+                            mac(tl, k, v_a[:, b * NT + cc * TPC + tl - OFFS[k] // P, :])
+                grs = [shifted_groups(nv) for nv in nvs]
+                for gi in range(max(len(g) for g in grs)):
+                    vos = []
+                    for tl, g in zip(tls, grs):
+                        if gi < len(g):
+                            vo = ps_ko.tile([P, 4, P], F32, name="vo", tag="ko")
+                            for i, s in enumerate(g[gi]):
+                                cl = WIN + tl * P - OFFS[s]
+                                nc.tensor.transpose(out=vo[:, i, :], in_=vwc[:, cl:cl + P], identity=ident[:])
+                            vos.append((tl, vo, g[gi]))
+                    for i in range(4):
+                        for tl, vo, gl in vos:
+                            if i < len(gl):
+                                mac(tl, gl[i], vo[:, i, :])
+            if pair == 1:
+                n0 = cc * CH
+                nc.sync.dma_start(out=out[b, n0:n0 + CH, :].rearrange("(t p) e -> p t e", p=P), in_=acc[:])
+
+        def ok(c):
+            return 0 <= c < NCHUNK
+
+        def body():
+            fe_load(0)
+            fe_load(1)
+            for c in range(-2, NCHUNK + 2):
+                for tl in range(TPC):
+                    if tl == 0 and ok(c + 3) and c + 3 >= 2:
+                        fe_load(c + 3)
+                    if ok(c + 2):
+                        fe_xpose(c + 2, tl)
+                    if ok(c + 1):
+                        if tl == 0:
+                            fe_quant(c + 1)
+                        if tl == 1:
+                            fe_kv(c + 1)
+                        if tl == 2:
+                            fe_q(c + 1)
+                            fe_ka(c + 1)
+                    if ok(c):
+                        scores(c, tl)
+                    if tl == 1:
+                        if ok(c - 2):
+                            values(c - 2, 1)
+                        if ok(c - 1):
+                            col_of[c - 1] = weights(c - 1)
+                    if tl == 3 and ok(c - 1):
+                        values(c - 1, 0)
+
+        if PINNED:
+            with tc.manual_schedule():
+                body()
+        else:
+            body()

@@ -26,8 +26,15 @@ OFFS = tuple(sorted([0] + [1 << i for i in range(12)] + [3 << j for j in range(1
 NOFF = 24
 NTAP = 45
 FLOPS = 2 * B * N * D * 3 * E + 4 * B * H * N * HD * NOFF
-ACT_SHARE = (0, 2, 4, 6)
-PINNED = False
+NEAR = 15
+ROW = 2 * P + 1
+UNIT = P * ROW
+WINV = 64
+VRING = 48
+BRING = 16
+NSLOT = 2
+SCR0 = B * N * E - NSLOT * 4 * UNIT
+HOLD0 = SCR0 // (CH * E)
 
 
 def n_valid(t):
@@ -50,7 +57,8 @@ def tile_dwarfattention_pa_t_kernel(tc, x, W_qkv, b_qkv, gains, pos_bias, identi
         const = ctx.enter_context(tc.tile_pool(name="const", bufs=1))
         ps_xt = ctx.enter_context(tc.psum_pool(name="ps_xt", bufs=2))
         ps_mm = ctx.enter_context(tc.psum_pool(name="ps_mm", bufs=2))
-        ps_ko = ctx.enter_context(tc.psum_pool(name="ps_ko", bufs=4))
+        ps_ko = ctx.enter_context(tc.psum_pool(name="ps_ko", bufs=3))
+        ps_acc = ctx.enter_context(tc.psum_pool(name="ps_acc", bufs=1))
 
         ident = const.tile([P, P], F32, name="ident")
         make_identity(nc, ident[:])
@@ -60,9 +68,15 @@ def tile_dwarfattention_pa_t_kernel(tc, x, W_qkv, b_qkv, gains, pos_bias, identi
         bias_col = const.tile([P, 4], F32, name="bias_col")
         bq_bc = const.tile([P, E], F32, name="bq_bc")
         pb_bc = const.tile([P, H, NTAP], F32, name="pb_bc")
-        gc = const.tile([P, B, H, NT, NTAP], F32, name="gc")
-        k_a = const.tile([P, B * NT, E], F32, name="k_a")
-        v_a = const.tile([P, B * NT, E], F32, name="v_a")
+        g_raw = const.tile([P, B, H, NT, NS], BF16, name="g_raw")
+        sp = const.tile([P, H], F32, name="sp")
+        k_a = const.tile([P, NT, E], F32, name="k_a")
+        v_a = const.tile([P, VRING, E], F32, name="v_a")
+        v_b = const.tile([P, BRING, E], F32, name="v_b")
+        held = const.tile([P, (NCHUNK - HOLD0) * TPC, E], F32, name="held")
+        d_rows = [const.tile([P, H, 2, ROW], F32, name="d_rows%d" % i) for i in range(NSLOT)]
+        for d_t in d_rows:
+            nc.gpsimd.memset(d_t[:], 0.0)
         junk = const.tile([P, HD], F32, name="junk")
 
         with tc.tile_pool(name="setup", bufs=1) as setup:
@@ -77,7 +91,6 @@ def tile_dwarfattention_pa_t_kernel(tc, x, W_qkv, b_qkv, gains, pos_bias, identi
             nc.scalar.dma_start(out=pb_raw[:], in_=pos_bias.rearrange("r h -> (r h)").partition_broadcast(P))
             ib_raw = setup.tile([P, H], BF16, name="ib_raw")
             nc.scalar.dma_start(out=ib_raw[:], in_=identity_bypass.partition_broadcast(P))
-            g_raw = setup.tile([P, B, H, NT, NS], BF16, name="g_raw")
             for b in range(B):
                 for h in range(H):
                     nc.scalar.dma_start(out=g_raw[:, b, h, :, :], in_=gains[b, h].rearrange("(t p) j -> p t j", p=P))
@@ -115,24 +128,15 @@ def tile_dwarfattention_pa_t_kernel(tc, x, W_qkv, b_qkv, gains, pos_bias, identi
             nc.scalar.activation(out=ib_e[:], in_=ib_e[:], func=ACTF.Exp, scale=-1.0)
             nc.vector.tensor_scalar_add(out=ib_e[:], in0=ib_e[:], scalar1=1.0)
             nc.scalar.activation(out=ib_e[:], in_=ib_e[:], func=ACTF.Ln)
-            sp = setup.tile([P, H], F32, name="sp")
             nc.vector.scalar_tensor_tensor(out=sp[:], in0=ib[:], scalar=0.0, in1=ib_e[:], op0=ALU.max, op1=ALU.add)
 
-            gcv = gc[:].rearrange("p b h t k -> p (b h t) k")
-            grv = g_raw[:].rearrange("p b h t j -> p (b h t) j")
-            for tau in range(4):
-                nc.gpsimd.tensor_scalar(out=gcv[:, :, 1 + NS * tau:1 + NS * (tau + 1)], in0=grv,
-                                        scalar1=D4[tau], scalar2=0.0, op0=ALU.mult, op1=ALU.add)
-            for b in range(B):
-                for h in range(H):
-                    nc.gpsimd.tensor_copy(out=gc[:, b, h, :, 0:1],
-                                          in_=sp[:, h:h + 1].unsqueeze(1).to_broadcast([P, NT, 1]))
 
         xp = ctx.enter_context(tc.tile_pool(name="xp", bufs=2))
         gp = ctx.enter_context(tc.tile_pool(name="gp", bufs=2))
         cp = ctx.enter_context(tc.tile_pool(name="cp", bufs=2))
         kwp = ctx.enter_context(tc.tile_pool(name="kwp", bufs=3))
-        vwp = ctx.enter_context(tc.tile_pool(name="vwp", bufs=5))
+        vwp = ctx.enter_context(tc.tile_pool(name="vwp", bufs=3))
+        ap_pool = ctx.enter_context(tc.tile_pool(name="ap_pool", bufs=2))
         qp = ctx.enter_context(tc.tile_pool(name="qp", bufs=3))
         pp = ctx.enter_context(tc.tile_pool(name="pp", bufs=3))
         sp_pool = ctx.enter_context(tc.tile_pool(name="sp_pool", bufs=3))
@@ -147,7 +151,7 @@ def tile_dwarfattention_pa_t_kernel(tc, x, W_qkv, b_qkv, gains, pos_bias, identi
         def window(c):
             if c not in kw:
                 kw[c] = kwp.tile([P, WIN + CH], F32, name="kw")
-                vw[c] = vwp.tile([P, WIN + CH], F32, name="vw")
+                vw[c] = vwp.tile([P, WINV + CH], F32, name="vw")
             return kw[c], vw[c]
 
         x_of = {}
@@ -187,19 +191,19 @@ def tile_dwarfattention_pa_t_kernel(tc, x, W_qkv, b_qkv, gains, pos_bias, identi
             kwc, vwc = window(c)
             if cc == 0:
                 nc.gpsimd.memset(kwc[:, 0:WIN], 0.0)
-                nc.gpsimd.memset(vwc[:, 0:WIN], 0.0)
-            for f, dst in ((1, kwc), (2, vwc)):
+                nc.gpsimd.memset(vwc[:, 0:WINV], 0.0)
+            for f, dst, win in ((1, kwc, WIN), (2, vwc, WINV)):
                 ps = ps_mm.tile([P, CH], F32, name="ps", tag="mm")
                 for g in range(2):
                     nc.tensor.matmul_mx(out=ps[:], lhsT=wc[:, g, f * P:(f + 1) * P].bitcast(FP8X4),
                                         lhsT_scale=ws[:, g, f * P:(f + 1) * P],
                                         rhs=codes[:, g, :].bitcast(FP8X4), rhs_scale=scl[:, g, :],
                                         start=(g == 0), stop=(g == 1))
-                nc.scalar.activation(out=dst[:, WIN:WIN + CH], in_=ps[:], func=ACTF.Identity,
+                nc.scalar.activation(out=dst[:, win:win + CH], in_=ps[:], func=ACTF.Identity,
                                      bias=bias_col[:, f:f + 1], scale=1.0)
                 if cc + 1 < NCC:
                     nxt = window(c + 1)[f - 1]
-                    nc.scalar.activation(out=nxt[:, 0:WIN], in_=ps[:, CH - WIN:CH], func=ACTF.Identity,
+                    nc.scalar.activation(out=nxt[:, 0:win], in_=ps[:, CH - win:CH], func=ACTF.Identity,
                                          bias=bias_col[:, f:f + 1], scale=1.0)
 
         def fe_q(c):
@@ -218,12 +222,14 @@ def tile_dwarfattention_pa_t_kernel(tc, x, W_qkv, b_qkv, gains, pos_bias, identi
 
         def fe_ka(c):
             b, cc = divmod(c, NCC)
-            for src, dst in ((kw[c], k_a), (vw[c], v_a)):
+            g0 = c * TPC
+            for src, first, dst, at in ((kw[c], WIN, k_a, cc * TPC), (vw[c], WINV, v_a, g0 % VRING),
+                                        (vw[c], 0, v_b, g0 % BRING)):
                 ta = ps_xt.tile([P, TPC, P], F32, name="ta", tag="xt")
                 for tl in range(TPC):
-                    nc.tensor.transpose(out=ta[:, tl, :], in_=src[:, WIN + tl * P:WIN + (tl + 1) * P],
+                    nc.tensor.transpose(out=ta[:, tl, :], in_=src[:, first + tl * P:first + (tl + 1) * P],
                                         identity=ident[:])
-                nc.scalar.copy(out=dst[:, b * NT + cc * TPC:b * NT + (cc + 1) * TPC, :], in_=ta[:])
+                nc.scalar.copy(out=dst[:, at:at + TPC, :], in_=ta[:])
 
         def shifted_groups(nv):
             una = [s for s in range(nv) if OFFS[s] % P != 0]
@@ -252,9 +258,9 @@ def tile_dwarfattention_pa_t_kernel(tc, x, W_qkv, b_qkv, gains, pos_bias, identi
                                                 in1=qb.unsqueeze(1).to_broadcast([P, ln, E]), op=ALU.mult)
                 for s in range(nv):
                     if OFFS[s] % P == 0:
-                        nc.vector.tensor_tensor(out=prod[:, s, :], in0=k_a[:, b * NT + t - OFFS[s] // P, :],
+                        nc.vector.tensor_tensor(out=prod[:, s, :], in0=k_a[:, t - OFFS[s] // P, :],
                                                 in1=qb, op=ALU.mult)
-                if (c * TPC + tl) % 7 in ACT_SHARE:
+                if True:
                     for s in range(nv):
                         for h in range(H):
                             nc.scalar.activation(out=junk[:], in_=prod[:, s, h * HD:(h + 1) * HD], func=ACTF.Copy,
@@ -289,8 +295,15 @@ def tile_dwarfattention_pa_t_kernel(tc, x, W_qkv, b_qkv, gains, pos_bias, identi
             nc.scalar.activation(out=e[:], in_=e[:], func=ACTF.Exp)
             nc.scalar.activation(out=u[:], in_=u[:], func=ACTF.Relu)
             nc.gpsimd.tensor_tensor(out=e[:], in0=e[:], in1=u[:], op=ALU.add)
+            gcc = cm.tile(shp, F32, name="gcc")
+            for tau in range(4):
+                nc.gpsimd.tensor_scalar(out=gcc[:, :, :, 1 + NS * tau:1 + NS * (tau + 1)],
+                                        in0=g_raw[:, b, :, cc * TPC:(cc + 1) * TPC, :],
+                                        scalar1=D4[tau], scalar2=0.0, op0=ALU.mult, op1=ALU.add)
+            nc.gpsimd.tensor_copy(out=gcc[:, :, :, 0:1],
+                                  in_=sp[:].unsqueeze(2).unsqueeze(3).to_broadcast([P, H, TPC, 1]))
             wt = cm.tile(shp, F32, name="wt")
-            nc.gpsimd.tensor_tensor(out=wt[:], in0=e[:], in1=gc[:, b, :, cc * TPC:(cc + 1) * TPC, :], op=ALU.mult)
+            nc.gpsimd.tensor_tensor(out=wt[:], in0=e[:], in1=gcc[:], op=ALU.mult)
             z1 = cm.tile([P, H, TPC], F32, name="z1")
             z3 = cm.tile([P, H, TPC], F32, name="z3")
             nc.vector.tensor_reduce(out=z1[:], in_=wt[:], axis=AX.X, op=ALU.add)
@@ -305,97 +318,138 @@ def tile_dwarfattention_pa_t_kernel(tc, x, W_qkv, b_qkv, gains, pos_bias, identi
             wp = cm.tile([P, H, TPC, 10], F32, name="wp")
             nc.gpsimd.tensor_tensor(out=wp[:], in0=wn[:, :, :, 13:23], in1=wn[:, :, :, 23:33], op=ALU.add)
 
-            def col(s, h, tl):
+            def place(s):
                 if s == 0:
-                    return w0[:, h, tl:tl + 1]
+                    return w0, None
                 if s == 1:
-                    return wn[:, h, tl, 12:13]
+                    return wn, 12
                 if s % 2 == 0:
-                    i = s // 2
-                    if i <= 10:
-                        return wp[:, h, tl, i - 1:i]
-                    return wn[:, h, tl, 33:34]
-                j = (s - 3) // 2
-                return wn[:, h, tl, 34 + j:35 + j]
+                    if s // 2 <= 10:
+                        return wp, s // 2 - 1
+                    return wn, 33
+                return wn, 34 + (s - 3) // 2
 
-            return col
+            def col(s, h, tl):
+                src, k = place(s)
+                if k is None:
+                    return src[:, h, tl:tl + 1]
+                return src[:, h, tl, k:k + 1]
 
-        acc_of = {}
+            def cols(s, tl0):
+                src, k = place(s)
+                if k is None:
+                    return src[:, :, tl0:tl0 + 2]
+                return src[:, :, tl0:tl0 + 2, k]
+
+            return col, cols
+
         col_of = {}
+        a_of = {}
+        at_of = {}
+        o_of = {}
+        scr = out.rearrange("b n e -> (b n e)")
 
-        def values(c, pair):
+        def skew(c, hc):
+            cols = col_of[c][1]
+            slot = (2 * c + hc) % NSLOT
+            d_t = d_rows[slot]
+            for s in range(NEAR):
+                nc.gpsimd.tensor_copy(out=d_t[:, :, :, P - OFFS[s]], in_=cols(s, 2 * hc))
+            area = scr[SCR0 + slot * 4 * UNIT:SCR0 + (slot + 1) * 4 * UNIT]
+            nc.sync.dma_start(out=area.rearrange("(u p w) -> p u w", u=4, p=P),
+                              in_=d_t[:].rearrange("p h t w -> p (h t) w"))
+            a_t = ap_pool.tile([P, 4, 2 * P], F32, name="a_t")
+            nc.sync.dma_start(out=a_t[:], in_=area.rearrange("(u r) -> u r", u=4)[:, 0:2 * P * P]
+                              .rearrange("u (p m) -> p u m", p=P))
+            a_of[(c, hc)] = a_t
+
+        def prep(c, hc):
+            a_t = a_of[(c, hc)]
+            at_t = ap_pool.tile([P, 8, P], F32, name="at_t")
+            for half in range(2):
+                tp = ps_xt.tile([P, 4, P], F32, name="tp", tag="xt")
+                for i in range(4):
+                    u, kb = divmod(4 * half + i, 2)
+                    nc.tensor.transpose(out=tp[:, i, :], in_=a_t[:, u, kb * P:(kb + 1) * P], identity=ident[:])
+                nc.scalar.copy(out=at_t[:, 4 * half:4 * half + 4, :], in_=tp[:])
+            at_of[(c, hc)] = at_t
+
+        def av(c, hc):
             b, cc = divmod(c, NCC)
-            vwc = vw[c]
-            col = col_of[c]
-            if pair == 0:
-                acc_of[c] = accp.tile([P, TPC, E], F32, name="acc")
-            acc = acc_of[c]
-
-            def mac(tl, s, src):
-                for h in range(H):
-                    hs = slice(h * HD, (h + 1) * HD)
-                    if s == 0:
-                        nc.vector.tensor_scalar_mul(out=acc[:, tl, hs], in0=src[:, hs], scalar1=col(s, h, tl))
-                    else:
-                        nc.vector.scalar_tensor_tensor(out=acc[:, tl, hs], in0=src[:, hs], scalar=col(s, h, tl),
-                                                       in1=acc[:, tl, hs], op0=ALU.mult, op1=ALU.add)
-
-            for tls in ((2 * pair, 2 * pair + 1),):
-                nvs = [n_valid(cc * TPC + tl) for tl in tls]
-                for k in range(NOFF):
-                    for tl, nv in zip(tls, nvs):
-                        if k < nv and OFFS[k] % P == 0:
-                            mac(tl, k, v_a[:, b * NT + cc * TPC + tl - OFFS[k] // P, :])
-                grs = [shifted_groups(nv) for nv in nvs]
-                for gi in range(max(len(g) for g in grs)):
-                    vos = []
-                    for tl, g in zip(tls, grs):
-                        if gi < len(g):
-                            vo = ps_ko.tile([P, 4, P], F32, name="vo", tag="ko")
-                            for i, s in enumerate(g[gi]):
-                                cl = WIN + tl * P - OFFS[s]
-                                nc.tensor.transpose(out=vo[:, i, :], in_=vwc[:, cl:cl + P], identity=ident[:])
-                            vos.append((tl, vo, g[gi]))
-                    for i in range(4):
-                        for tl, vo, gl in vos:
-                            if i < len(gl):
-                                mac(tl, gl[i], vo[:, i, :])
-            if pair == 1:
+            col = col_of[c][0]
+            at_t = at_of[(c, hc)]
+            if hc == 0:
+                if c >= HOLD0:
+                    o_of[c] = held[:, (c - HOLD0) * TPC:(c - HOLD0 + 1) * TPC, :]
+                else:
+                    o_of[c] = accp.tile([P, TPC, E], F32, name="o_sb")
+            o_sb = o_of[c]
+            near = ps_acc.tile([P, 4, HD], F32, name="near")
+            for h in range(H):
+                for t2 in range(2):
+                    u = 2 * h + t2
+                    t = cc * TPC + 2 * hc + t2
+                    g = c * TPC + 2 * hc + t2
+                    kbs = [kb for kb in range(2) if t - 1 + kb >= 0]
+                    for kb in kbs:
+                        nc.tensor.matmul(out=near[:, u, :], lhsT=at_t[:, 2 * u + kb, :],
+                                         rhs=v_a[:, (g - 1 + kb) % VRING, h * HD:(h + 1) * HD],
+                                         start=(kb == kbs[0]), stop=(kb == kbs[-1]))
+            for k in range(NEAR, NOFF + 1):
+                for t2 in range(2):
+                    tl = 2 * hc + t2
+                    t = cc * TPC + tl
+                    g = c * TPC + tl
+                    nv = n_valid(t)
+                    for h in range(H):
+                        hs = slice(h * HD, (h + 1) * HD)
+                        prev = near[:, 2 * h + t2, :] if k == NEAR else o_sb[:, tl, hs]
+                        if k < nv:
+                            if OFFS[k] % P == 0:
+                                src = v_a[:, (g - OFFS[k] // P) % VRING, hs]
+                            else:
+                                src = v_b[:, (g - 1) % BRING, hs]
+                            nc.vector.scalar_tensor_tensor(out=o_sb[:, tl, hs], in0=src, scalar=col(k, h, tl),
+                                                           in1=prev, op0=ALU.mult, op1=ALU.add)
+                        elif k == NEAR:
+                            nc.vector.tensor_copy(out=o_sb[:, tl, hs], in_=prev)
+            if hc == 1 and c < HOLD0:
                 n0 = cc * CH
-                nc.sync.dma_start(out=out[b, n0:n0 + CH, :].rearrange("(t p) e -> p t e", p=P), in_=acc[:])
+                nc.sync.dma_start(out=out[b, n0:n0 + CH, :].rearrange("(t p) e -> p t e", p=P), in_=o_sb[:])
 
         def ok(c):
             return 0 <= c < NCHUNK
 
-        def body():
-            fe_load(0)
-            fe_load(1)
-            for c in range(-2, NCHUNK + 2):
-                for tl in range(TPC):
-                    if tl == 0 and ok(c + 3) and c + 3 >= 2:
-                        fe_load(c + 3)
-                    if ok(c + 2):
-                        fe_xpose(c + 2, tl)
-                    if ok(c + 1):
-                        if tl == 0:
-                            fe_quant(c + 1)
-                        if tl == 1:
-                            fe_kv(c + 1)
-                        if tl == 2:
-                            fe_q(c + 1)
-                            fe_ka(c + 1)
-                    if ok(c):
-                        scores(c, tl)
+        fe_load(0)
+        fe_load(1)
+        for c in range(-2, NCHUNK + 3):
+            for tl in range(TPC):
+                if tl == 0 and ok(c + 3) and c + 3 >= 2:
+                    fe_load(c + 3)
+                if ok(c + 2):
+                    fe_xpose(c + 2, tl)
+                if ok(c + 1):
+                    if tl == 0:
+                        fe_quant(c + 1)
                     if tl == 1:
-                        if ok(c - 2):
-                            values(c - 2, 1)
-                        if ok(c - 1):
-                            col_of[c - 1] = weights(c - 1)
-                    if tl == 3 and ok(c - 1):
-                        values(c - 1, 0)
-
-        if PINNED:
-            with tc.manual_schedule():
-                body()
-        else:
-            body()
+                        fe_kv(c + 1)
+                    if tl == 2:
+                        fe_q(c + 1)
+                        fe_ka(c + 1)
+                if ok(c):
+                    scores(c, tl)
+                if tl == 1 and ok(c - 1):
+                    col_of[c - 1] = weights(c - 1)
+                    skew(c - 1, 0)
+                    skew(c - 1, 1)
+                if tl == 3 and ok(c - 1):
+                    prep(c - 1, 0)
+                if tl == 0 and ok(c - 2):
+                    prep(c - 2, 1)
+                    av(c - 2, 0)
+                if tl == 1 and ok(c - 2):
+                    av(c - 2, 1)
+        for c in range(HOLD0, NCHUNK):
+            b, cc = divmod(c, NCC)
+            nc.sync.dma_start(out=out[b, cc * CH:(cc + 1) * CH, :].rearrange("(t p) e -> p t e", p=P),
+                              in_=held[:, (c - HOLD0) * TPC:(c - HOLD0 + 1) * TPC, :])

@@ -26,6 +26,7 @@ OFFS = tuple(sorted([0] + [1 << i for i in range(12)] + [3 << j for j in range(1
 NOFF = 24
 NTAP = 45
 FLOPS = 2 * B * N * D * 3 * E + 4 * B * H * N * HD * NOFF
+REDUCER = "V"
 NEAR = 15
 ROW = 2 * P + 1
 UNIT = P * ROW
@@ -260,19 +261,15 @@ def tile_dwarfattention_pa_t_kernel(tc, x, W_qkv, b_qkv, gains, pos_bias, identi
                     if OFFS[s] % P == 0:
                         nc.vector.tensor_tensor(out=prod[:, s, :], in0=k_a[:, t - OFFS[s] // P, :],
                                                 in1=qb, op=ALU.mult)
-                if True:
+                if REDUCER[(c * TPC + tl) % len(REDUCER)] == "S":
                     for s in range(nv):
                         for h in range(H):
                             nc.scalar.activation(out=junk[:], in_=prod[:, s, h * HD:(h + 1) * HD], func=ACTF.Copy,
                                                  accum_out=s_t[:, h, tl, s:s + 1])
                 else:
-                    pv = prod[:, 0:nv, :].rearrange("p s (h d) -> p (s h) d", h=H)
-                    for w in (32, 16, 8, 4, 2):
-                        nc.gpsimd.tensor_tensor(out=pv[:, :, 0:w], in0=pv[:, :, 0:w], in1=pv[:, :, w:2 * w],
-                                                op=ALU.add)
-                    p4 = prod[:, 0:nv, :].rearrange("p s (h d) -> p s h d", h=H)
-                    nc.gpsimd.tensor_tensor(out=s_t[:, :, tl, 0:nv].rearrange("p h s -> p s h"),
-                                            in0=p4[:, :, :, 0], in1=p4[:, :, :, 1], op=ALU.add)
+                    nc.vector.tensor_reduce(out=s_t[:, :, tl, 0:nv].rearrange("p h s -> p s h"),
+                                            in_=prod[:, 0:nv, :].rearrange("p s (h d) -> p s h d", h=H),
+                                            axis=AX.X, op=ALU.add)
 
         def weights(c):
             b, cc = divmod(c, NCC)
@@ -291,17 +288,16 @@ def tile_dwarfattention_pa_t_kernel(tc, x, W_qkv, b_qkv, gains, pos_bias, identi
             nc.gpsimd.tensor_tensor(out=u[:, :, :, 23:34], in0=spair[:, :, :, 0:11, 0], in1=pbs(23, 34), op=ALU.add)
             nc.gpsimd.tensor_tensor(out=u[:, :, :, 34:45], in0=spair[:, :, :, 0:11, 1], in1=pbs(34, 45), op=ALU.add)
             e = cm.tile(shp, F32, name="e")
-            nc.gpsimd.tensor_scalar(out=e[:], in0=u[:], scalar1=0.0, scalar2=0.0, op0=ALU.min, op1=ALU.add)
-            nc.scalar.activation(out=e[:], in_=e[:], func=ACTF.Exp)
+            nc.scalar.activation(out=e[:], in_=u[:], func=ACTF.Exp)
             nc.scalar.activation(out=u[:], in_=u[:], func=ACTF.Relu)
-            nc.gpsimd.tensor_tensor(out=e[:], in0=e[:], in1=u[:], op=ALU.add)
+            nc.vector.scalar_tensor_tensor(out=e[:].rearrange("p h t k -> p (h t k)"),
+                                           in0=e[:].rearrange("p h t k -> p (h t k)"), scalar=1.0,
+                                           in1=u[:].rearrange("p h t k -> p (h t k)"), op0=ALU.min, op1=ALU.add)
             gcc = cm.tile(shp, F32, name="gcc")
             for tau in range(4):
-                nc.gpsimd.tensor_scalar(out=gcc[:, :, :, 1 + NS * tau:1 + NS * (tau + 1)],
-                                        in0=g_raw[:, b, :, cc * TPC:(cc + 1) * TPC, :],
-                                        scalar1=D4[tau], scalar2=0.0, op0=ALU.mult, op1=ALU.add)
-            nc.gpsimd.tensor_copy(out=gcc[:, :, :, 0:1],
-                                  in_=sp[:].unsqueeze(2).unsqueeze(3).to_broadcast([P, H, TPC, 1]))
+                nc.scalar.activation(out=gcc[:, :, :, 1 + NS * tau:1 + NS * (tau + 1)],
+                                     in_=g_raw[:, b, :, cc * TPC:(cc + 1) * TPC, :], func=ACTF.Copy, scale=D4[tau])
+            nc.scalar.copy(out=gcc[:, :, :, 0:1], in_=sp[:].unsqueeze(2).unsqueeze(3).to_broadcast([P, H, TPC, 1]))
             wt = cm.tile(shp, F32, name="wt")
             nc.gpsimd.tensor_tensor(out=wt[:], in0=e[:], in1=gcc[:], op=ALU.mult)
             z1 = cm.tile([P, H, TPC], F32, name="z1")
@@ -354,7 +350,7 @@ def tile_dwarfattention_pa_t_kernel(tc, x, W_qkv, b_qkv, gains, pos_bias, identi
             slot = (2 * c + hc) % NSLOT
             d_t = d_rows[slot]
             for s in range(NEAR):
-                nc.gpsimd.tensor_copy(out=d_t[:, :, :, P - OFFS[s]], in_=cols(s, 2 * hc))
+                nc.scalar.copy(out=d_t[:, :, :, P - OFFS[s]], in_=cols(s, 2 * hc))
             area = scr[SCR0 + slot * 4 * UNIT:SCR0 + (slot + 1) * 4 * UNIT]
             nc.sync.dma_start(out=area.rearrange("(u p w) -> p u w", u=4, p=P),
                               in_=d_t[:].rearrange("p h t w -> p (h t) w"))

@@ -26,7 +26,7 @@ OFFS = tuple(sorted([0] + [1 << i for i in range(12)] + [3 << j for j in range(1
 NOFF = 24
 NTAP = 45
 FLOPS = 2 * B * N * D * 3 * E + 4 * B * H * N * HD * NOFF
-REDUCER = "V"
+REDUCER = "VVG"
 NEAR = 15
 ROW = 2 * P + 1
 UNIT = P * ROW
@@ -261,11 +261,14 @@ def tile_dwarfattention_pa_t_kernel(tc, x, W_qkv, b_qkv, gains, pos_bias, identi
                     if OFFS[s] % P == 0:
                         nc.vector.tensor_tensor(out=prod[:, s, :], in0=k_a[:, t - OFFS[s] // P, :],
                                                 in1=qb, op=ALU.mult)
-                if REDUCER[(c * TPC + tl) % len(REDUCER)] == "S":
-                    for s in range(nv):
-                        for h in range(H):
-                            nc.scalar.activation(out=junk[:], in_=prod[:, s, h * HD:(h + 1) * HD], func=ACTF.Copy,
-                                                 accum_out=s_t[:, h, tl, s:s + 1])
+                if REDUCER[(c * TPC + tl) % len(REDUCER)] == "G":
+                    pv = prod[:, 0:nv, :].rearrange("p s (h d) -> p (s h) d", h=H)
+                    for w in (32, 16, 8, 4, 2):
+                        nc.gpsimd.tensor_tensor(out=pv[:, :, 0:w], in0=pv[:, :, 0:w], in1=pv[:, :, w:2 * w],
+                                                op=ALU.add)
+                    p4 = prod[:, 0:nv, :].rearrange("p s (h d) -> p s h d", h=H)
+                    nc.gpsimd.tensor_tensor(out=s_t[:, :, tl, 0:nv].rearrange("p h s -> p s h"),
+                                            in0=p4[:, :, :, 0], in1=p4[:, :, :, 1], op=ALU.add)
                 else:
                     nc.vector.tensor_reduce(out=s_t[:, :, tl, 0:nv].rearrange("p h s -> p s h"),
                                             in_=prod[:, 0:nv, :].rearrange("p s (h d) -> p s h d", h=H),

@@ -26,7 +26,8 @@ OFFS = tuple(sorted([0] + [1 << i for i in range(12)] + [3 << j for j in range(1
 NOFF = 24
 NTAP = 45
 FLOPS = 2 * B * N * D * 3 * E + 4 * B * H * N * HD * NOFF
-REDUCER = "VVG"
+REDUCER = "VP"
+A = 32
 NEAR = 15
 ROW = 2 * P + 1
 UNIT = P * ROW
@@ -57,17 +58,22 @@ def tile_dwarfattention_pa_t_kernel(tc, x, W_qkv, b_qkv, gains, pos_bias, identi
     with ExitStack() as ctx:
         const = ctx.enter_context(tc.tile_pool(name="const", bufs=1))
         ps_xt = ctx.enter_context(tc.psum_pool(name="ps_xt", bufs=2))
-        ps_mm = ctx.enter_context(tc.psum_pool(name="ps_mm", bufs=2))
+        ps_mm = ctx.enter_context(tc.psum_pool(name="ps_mm", bufs=1))
+        ps_st = ctx.enter_context(tc.psum_pool(name="ps_st", bufs=1))
         ps_ko = ctx.enter_context(tc.psum_pool(name="ps_ko", bufs=3))
         ps_acc = ctx.enter_context(tc.psum_pool(name="ps_acc", bufs=1))
 
         ident = const.tile([P, P], F32, name="ident")
         make_identity(nc, ident[:])
+        perm = const.tile([P, P], F32, name="perm")
+        nc.vector.tensor_copy(out=perm[:].rearrange("p (a h e) -> p a h e", a=A, h=H),
+                              in_=ident[:].rearrange("p (h a e) -> p a h e", h=H, a=A))
+        pbuf = const.tile([P, A, P], F32, name="pbuf")
+        nc.vector.memset(pbuf[:], 0.0)
 
         wc = const.tile([P, 2, 3 * P], U32, name="wc", align_bytes=64)
         ws = const.tile([P, 2, 3 * P], U8, name="ws", align_bytes=64)
         bias_col = const.tile([P, 4], F32, name="bias_col")
-        bq_bc = const.tile([P, E], F32, name="bq_bc")
         pb_bc = const.tile([P, H, NTAP], F32, name="pb_bc")
         g_raw = const.tile([P, B, H, NT, NS], BF16, name="g_raw")
         sp = const.tile([P, H], F32, name="sp")
@@ -86,8 +92,6 @@ def tile_dwarfattention_pa_t_kernel(tc, x, W_qkv, b_qkv, gains, pos_bias, identi
             b_rows = setup.tile([P, P], BF16, name="b_rows")
             nc.vector.memset(b_rows[:], 0.0)
             nc.scalar.dma_start(out=b_rows[0:3, :], in_=b_qkv.rearrange("(f c) -> f c", c=P))
-            bq_raw = setup.tile([P, E], BF16, name="bq_raw")
-            nc.scalar.dma_start(out=bq_raw[:], in_=b_qkv[0:E].partition_broadcast(P))
             pb_raw = setup.tile([P, 4 * NS * H], BF16, name="pb_raw")
             nc.scalar.dma_start(out=pb_raw[:], in_=pos_bias.rearrange("r h -> (r h)").partition_broadcast(P))
             ib_raw = setup.tile([P, H], BF16, name="ib_raw")
@@ -116,7 +120,6 @@ def tile_dwarfattention_pa_t_kernel(tc, x, W_qkv, b_qkv, gains, pos_bias, identi
             bt = ps_xt.tile([P, 4, P], F32, name="bt", tag="xt")
             nc.tensor.transpose(out=bt[:, 0, :], in_=b_rows32[:], identity=ident[:])
             nc.vector.tensor_copy(out=bias_col[:, 0:3], in_=bt[:, 0, 0:3])
-            nc.vector.tensor_copy(out=bq_bc[:], in_=bq_raw[:])
 
             nc.vector.memset(pb_bc[:], 0.0)
             nc.vector.tensor_copy(out=pb_bc[:, :, 1:NTAP].rearrange("p h (t j) -> p h t j", t=4),
@@ -139,14 +142,16 @@ def tile_dwarfattention_pa_t_kernel(tc, x, W_qkv, b_qkv, gains, pos_bias, identi
         vwp = ctx.enter_context(tc.tile_pool(name="vwp", bufs=3))
         ap_pool = ctx.enter_context(tc.tile_pool(name="ap_pool", bufs=2))
         qp = ctx.enter_context(tc.tile_pool(name="qp", bufs=3))
-        pp = ctx.enter_context(tc.tile_pool(name="pp", bufs=3))
+        pp = ctx.enter_context(tc.tile_pool(name="pp", bufs=2))
         sp_pool = ctx.enter_context(tc.tile_pool(name="sp_pool", bufs=3))
         cm = ctx.enter_context(tc.tile_pool(name="cm", bufs=3))
         accp = ctx.enter_context(tc.tile_pool(name="accp", bufs=2))
+        stp = ctx.enter_context(tc.tile_pool(name="stp", bufs=2))
 
         kw = {}
         vw = {}
         q_of = {}
+        q2_of = {}
         s_of = {}
 
         def window(c):
@@ -191,8 +196,8 @@ def tile_dwarfattention_pa_t_kernel(tc, x, W_qkv, b_qkv, gains, pos_bias, identi
             codes, scl = code_of[c]
             kwc, vwc = window(c)
             if cc == 0:
-                nc.gpsimd.memset(kwc[:, 0:WIN], 0.0)
-                nc.gpsimd.memset(vwc[:, 0:WINV], 0.0)
+                nc.vector.memset(kwc[:, 0:WIN], 0.0)
+                nc.vector.memset(vwc[:, 0:WINV], 0.0)
             for f, dst, win in ((1, kwc, WIN), (2, vwc, WINV)):
                 ps = ps_mm.tile([P, CH], F32, name="ps", tag="mm")
                 for g in range(2):
@@ -209,16 +214,24 @@ def tile_dwarfattention_pa_t_kernel(tc, x, W_qkv, b_qkv, gains, pos_bias, identi
 
         def fe_q(c):
             codes, scl = code_of[c]
-            psq = ps_mm.tile([P, TPC, E], F32, name="psq", tag="mm")
+            psq = ps_mm.tile([P, CH], F32, name="psq", tag="mm")
+            for g in range(2):
+                nc.tensor.matmul_mx(out=psq[:], lhsT=wc[:, g, 0:P].bitcast(FP8X4), lhsT_scale=ws[:, g, 0:P],
+                                    rhs=codes[:, g, :].bitcast(FP8X4), rhs_scale=scl[:, g, :],
+                                    start=(g == 0), stop=(g == 1))
+            q_t = qp.tile([P, CH], F32, name="q_t")
+            nc.scalar.activation(out=q_t[:], in_=psq[:], func=ACTF.Identity, bias=bias_col[:, 0:1], scale=1.0)
+            tq = ps_xt.tile([P, TPC, P], F32, name="tq", tag="xt")
             for tl in range(TPC):
-                for g in range(2):
-                    nc.tensor.matmul_mx(out=psq[:, tl, :], lhsT=codes[:, g, tl * P:(tl + 1) * P].bitcast(FP8X4),
-                                        lhsT_scale=scl[:, g, tl * P:(tl + 1) * P],
-                                        rhs=wc[:, g, 0:P].bitcast(FP8X4), rhs_scale=ws[:, g, 0:P],
-                                        start=(g == 0), stop=(g == 1))
+                nc.tensor.transpose(out=tq[:, tl, :], in_=q_t[:, tl * P:(tl + 1) * P], identity=ident[:])
             q_sb = qp.tile([P, TPC, E], F32, name="q_sb")
-            nc.vector.tensor_tensor(out=q_sb[:], in0=psq[:], in1=bq_bc[:].unsqueeze(1).to_broadcast([P, TPC, E]),
-                                    op=ALU.add)
+            nc.scalar.copy(out=q_sb[:], in_=tq[:])
+            tq2 = ps_xt.tile([P, TPC, P], F32, name="tq2", tag="xt")
+            for tl in range(TPC):
+                nc.tensor.transpose(out=tq2[:, tl, :], in_=q_t[:, tl * P:(tl + 1) * P], identity=perm[:])
+            q2_sb = qp.tile([P, TPC, E], F32, name="q2_sb")
+            nc.scalar.copy(out=q2_sb[:], in_=tq2[:])
+            q2_of[c] = q2_sb
             q_of[c] = q_sb
 
         def fe_ka(c):
@@ -243,10 +256,12 @@ def tile_dwarfattention_pa_t_kernel(tc, x, W_qkv, b_qkv, gains, pos_bias, identi
             if tl == 0:
                 s_of[c] = sp_pool.tile([P, H, TPC, NOFF], F32, name="s_t")
                 if n_valid(cc * TPC) < NOFF:
-                    nc.gpsimd.memset(s_of[c][:], 0.0)
+                    nc.vector.memset(s_of[c][:], 0.0)
             s_t = s_of[c]
-            for t in (cc * TPC + tl,):
-                nv = n_valid(t)
+            t = cc * TPC + tl
+            nv = n_valid(t)
+            s_out = s_t[:, :, tl, 0:nv].rearrange("p h s -> p s h")
+            if REDUCER[(c * TPC + tl) % len(REDUCER)] == "V":
                 prod = pp.tile([P, NOFF, E], F32, name="prod")
                 qb = q_sb[:, tl, :]
                 for grp_s in shifted_groups(nv):
@@ -261,18 +276,36 @@ def tile_dwarfattention_pa_t_kernel(tc, x, W_qkv, b_qkv, gains, pos_bias, identi
                     if OFFS[s] % P == 0:
                         nc.vector.tensor_tensor(out=prod[:, s, :], in0=k_a[:, t - OFFS[s] // P, :],
                                                 in1=qb, op=ALU.mult)
-                if REDUCER[(c * TPC + tl) % len(REDUCER)] == "G":
-                    pv = prod[:, 0:nv, :].rearrange("p s (h d) -> p (s h) d", h=H)
-                    for w in (32, 16, 8, 4, 2):
-                        nc.gpsimd.tensor_tensor(out=pv[:, :, 0:w], in0=pv[:, :, 0:w], in1=pv[:, :, w:2 * w],
-                                                op=ALU.add)
-                    p4 = prod[:, 0:nv, :].rearrange("p s (h d) -> p s h d", h=H)
-                    nc.gpsimd.tensor_tensor(out=s_t[:, :, tl, 0:nv].rearrange("p h s -> p s h"),
-                                            in0=p4[:, :, :, 0], in1=p4[:, :, :, 1], op=ALU.add)
-                else:
-                    nc.vector.tensor_reduce(out=s_t[:, :, tl, 0:nv].rearrange("p h s -> p s h"),
-                                            in_=prod[:, 0:nv, :].rearrange("p s (h d) -> p s h d", h=H),
-                                            axis=AX.X, op=ALU.add)
+                nc.vector.tensor_reduce(out=s_out, in_=prod[:, 0:nv, :].rearrange("p s (h d) -> p s h d", h=H),
+                                        axis=AX.X, op=ALU.add)
+            else:
+                q2 = q2_of[c][:, tl, :].rearrange("p (a k) -> p a k", k=4)
+                for grp_s in shifted_groups(nv):
+                    ko = ps_ko.tile([P, 4, P], F32, name="ko", tag="ko")
+                    for i, s in enumerate(grp_s):
+                        col = WIN + tl * P - OFFS[s]
+                        nc.tensor.transpose(out=ko[:, i, :], in_=kwc[:, col:col + P], identity=perm[:])
+                    for i0, s0, ln in runs_of(list(enumerate(grp_s))):
+                        nc.vector.tensor_tensor(
+                            out=pbuf[:, :, 4 * s0:4 * (s0 + ln)].rearrange("p a (s k) -> p a s k", k=4),
+                            in0=ko[:, i0:i0 + ln, :].rearrange("p s (a k) -> p a s k", k=4),
+                            in1=q2.unsqueeze(2).to_broadcast([P, A, ln, 4]), op=ALU.mult)
+                for s in range(nv):
+                    if OFFS[s] % P == 0:
+                        nc.vector.tensor_tensor(
+                            out=pbuf[:, :, 4 * s:4 * s + 4].rearrange("p a (h e) -> p a h e", h=H),
+                            in0=k_a[:, t - OFFS[s] // P, :].rearrange("p (h a e) -> p a h e", h=H, a=A),
+                            in1=q2.rearrange("p a (h e) -> p a h e", h=H), op=ALU.mult)
+                st = ps_st.tile([P, P], F32, name="st", tag="st")
+                for a in range(A):
+                    nc.tensor.matmul(out=st[:], lhsT=pbuf[:, a, :], rhs=ident[:], is_transpose=True,
+                                     start=(a == 0), stop=(a == A - 1))
+                st_sb = stp.tile([P, P], F32, name="st_sb")
+                nc.scalar.copy(out=st_sb[:], in_=st[:])
+                bk = ps_st.tile([P, P], F32, name="bk", tag="st")
+                nc.tensor.transpose(out=bk[:], in_=st_sb[:], identity=ident[:])
+                nc.vector.tensor_reduce(out=s_out, in_=bk[:, 0:4 * nv].rearrange("p (s h e) -> p s h e", h=H, e=2),
+                                        axis=AX.X, op=ALU.add)
 
         def weights(c):
             b, cc = divmod(c, NCC)
@@ -281,15 +314,12 @@ def tile_dwarfattention_pa_t_kernel(tc, x, W_qkv, b_qkv, gains, pos_bias, identi
             u = cm.tile(shp, F32, name="u")
             spair = s_t[:, :, :, 2:NOFF].rearrange("p h t (i two) -> p h t i two", two=2)
 
-            def pbs(lo, hi):
-                return pb_bc[:, :, lo:hi].unsqueeze(2).to_broadcast([P, H, TPC, hi - lo])
-
-            nc.gpsimd.tensor_tensor(out=u[:, :, :, 0:12], in0=s_t[:, :, :, 0:1].to_broadcast([P, H, TPC, 12]),
-                                    in1=pbs(0, 12), op=ALU.add)
-            nc.gpsimd.tensor_tensor(out=u[:, :, :, 12:13], in0=s_t[:, :, :, 1:2], in1=pbs(12, 13), op=ALU.add)
-            nc.gpsimd.tensor_tensor(out=u[:, :, :, 13:23], in0=spair[:, :, :, 0:10, 0], in1=pbs(13, 23), op=ALU.add)
-            nc.gpsimd.tensor_tensor(out=u[:, :, :, 23:34], in0=spair[:, :, :, 0:11, 0], in1=pbs(23, 34), op=ALU.add)
-            nc.gpsimd.tensor_tensor(out=u[:, :, :, 34:45], in0=spair[:, :, :, 0:11, 1], in1=pbs(34, 45), op=ALU.add)
+            nc.scalar.copy(out=u[:, :, :, 0:12], in_=s_t[:, :, :, 0:1].to_broadcast([P, H, TPC, 12]))
+            nc.scalar.copy(out=u[:, :, :, 12:13], in_=s_t[:, :, :, 1:2])
+            nc.scalar.copy(out=u[:, :, :, 13:23], in_=spair[:, :, :, 0:10, 0])
+            nc.scalar.copy(out=u[:, :, :, 23:34], in_=spair[:, :, :, 0:11, 0])
+            nc.scalar.copy(out=u[:, :, :, 34:45], in_=spair[:, :, :, 0:11, 1])
+            nc.vector.tensor_tensor(out=u[:], in0=u[:], in1=pb_bc[:].unsqueeze(2).to_broadcast(shp), op=ALU.add)
             e = cm.tile(shp, F32, name="e")
             nc.scalar.activation(out=e[:], in_=u[:], func=ACTF.Exp)
             nc.scalar.activation(out=u[:], in_=u[:], func=ACTF.Relu)
@@ -302,7 +332,7 @@ def tile_dwarfattention_pa_t_kernel(tc, x, W_qkv, b_qkv, gains, pos_bias, identi
                                      in_=g_raw[:, b, :, cc * TPC:(cc + 1) * TPC, :], func=ACTF.Copy, scale=D4[tau])
             nc.scalar.copy(out=gcc[:, :, :, 0:1], in_=sp[:].unsqueeze(2).unsqueeze(3).to_broadcast([P, H, TPC, 1]))
             wt = cm.tile(shp, F32, name="wt")
-            nc.gpsimd.tensor_tensor(out=wt[:], in0=e[:], in1=gcc[:], op=ALU.mult)
+            nc.vector.tensor_tensor(out=wt[:], in0=e[:], in1=gcc[:], op=ALU.mult)
             z1 = cm.tile([P, H, TPC], F32, name="z1")
             z3 = cm.tile([P, H, TPC], F32, name="z3")
             nc.vector.tensor_reduce(out=z1[:], in_=wt[:], axis=AX.X, op=ALU.add)
@@ -310,12 +340,11 @@ def tile_dwarfattention_pa_t_kernel(tc, x, W_qkv, b_qkv, gains, pos_bias, identi
             nc.vector.scalar_tensor_tensor(out=z1[:], in0=z3[:], scalar=-2.0, in1=z1[:], op0=ALU.mult, op1=ALU.add)
             nc.vector.tensor_scalar_add(out=z1[:], in0=z1[:], scalar1=1e-6)
             nc.vector.reciprocal(out=z3[:], in_=z1[:])
-            wn = cm.tile(shp, F32, name="wn")
-            nc.gpsimd.tensor_tensor(out=wn[:], in0=wt[:], in1=z3[:].unsqueeze(3).to_broadcast(shp), op=ALU.mult)
+            wn = wt
             w0 = cm.tile([P, H, TPC], F32, name="w0")
             nc.vector.tensor_reduce(out=w0[:], in_=wn[:, :, :, 0:12], axis=AX.X, op=ALU.add)
             wp = cm.tile([P, H, TPC, 10], F32, name="wp")
-            nc.gpsimd.tensor_tensor(out=wp[:], in0=wn[:, :, :, 13:23], in1=wn[:, :, :, 23:33], op=ALU.add)
+            nc.vector.tensor_tensor(out=wp[:], in0=wn[:, :, :, 13:23], in1=wn[:, :, :, 23:33], op=ALU.add)
 
             def place(s):
                 if s == 0:
@@ -340,7 +369,7 @@ def tile_dwarfattention_pa_t_kernel(tc, x, W_qkv, b_qkv, gains, pos_bias, identi
                     return src[:, :, tl0:tl0 + 2]
                 return src[:, :, tl0:tl0 + 2, k]
 
-            return col, cols
+            return col, cols, z3
 
         col_of = {}
         a_of = {}
@@ -412,6 +441,13 @@ def tile_dwarfattention_pa_t_kernel(tc, x, W_qkv, b_qkv, gains, pos_bias, identi
                                                            in1=prev, op0=ALU.mult, op1=ALU.add)
                         elif k == NEAR:
                             nc.vector.tensor_copy(out=o_sb[:, tl, hs], in_=prev)
+            rz = col_of[c][2]
+            for t2 in range(2):
+                tl = 2 * hc + t2
+                for h in range(H):
+                    hs = slice(h * HD, (h + 1) * HD)
+                    nc.scalar.activation(out=o_sb[:, tl, hs], in_=o_sb[:, tl, hs], func=ACTF.Copy,
+                                         scale=rz[:, h, tl:tl + 1])
             if hc == 1 and c < HOLD0:
                 n0 = cc * CH
                 nc.sync.dma_start(out=out[b, n0:n0 + CH, :].rearrange("(t p) e -> p t e", p=P), in_=o_sb[:])

@@ -20,36 +20,38 @@ TPC = CH // P
 NCC = N // CH
 NT = N // P
 NCHUNK = B * NCC
-WIN = 256
 D4 = (0.4829629131445341, 0.8365163037378079, 0.2241438680420134, -0.1294095225512604)
 OFFS = tuple(sorted([0] + [1 << i for i in range(12)] + [3 << j for j in range(11)]))
-NOFF = 24
-NTAP = 45
-FLOPS = 2 * B * N * D * 3 * E + 4 * B * H * N * HD * NOFF
-REDUCER = "VP"
-A = 32
+NOFF = len(OFFS)
+NTAP = 1 + 4 * NS
 NEAR = 15
+KWIN = 256
+VWIN = 64
 ROW = 2 * P + 1
 UNIT = P * ROW
-WINV = 64
 VRING = 48
 BRING = 16
-NSLOT = 2
-SCR0 = B * N * E - NSLOT * 4 * UNIT
+SCR0 = B * N * E - H * TPC * UNIT
 HOLD0 = SCR0 // (CH * E)
+FLOPS = 2 * B * N * D * 3 * E + 4 * B * H * N * HD * NOFF
 
 
 def n_valid(t):
     return len([o for o in OFFS if o <= t * P + P - 1])
 
 
-def runs_of(slots):
+def cut_groups(nv):
+    cut = [s for s in range(nv) if OFFS[s] % P != 0]
+    return [cut[i:i + 4] for i in range(0, len(cut), 4)]
+
+
+def runs_of(places):
     runs = []
-    for place, slot in slots:
-        if runs and runs[-1][0] + runs[-1][2] == place and runs[-1][1] + runs[-1][2] == slot:
+    for i, s in enumerate(places):
+        if runs and runs[-1][1] + runs[-1][2] == s:
             runs[-1][2] += 1
         else:
-            runs.append([place, slot, 1])
+            runs.append([i, s, 1])
     return runs
 
 
@@ -57,34 +59,26 @@ def tile_dwarfattention_pa_t_kernel(tc, x, W_qkv, b_qkv, gains, pos_bias, identi
     nc = tc.nc
     with ExitStack() as ctx:
         const = ctx.enter_context(tc.tile_pool(name="const", bufs=1))
-        ps_xt = ctx.enter_context(tc.psum_pool(name="ps_xt", bufs=2))
-        ps_mm = ctx.enter_context(tc.psum_pool(name="ps_mm", bufs=1))
-        ps_st = ctx.enter_context(tc.psum_pool(name="ps_st", bufs=1))
-        ps_ko = ctx.enter_context(tc.psum_pool(name="ps_ko", bufs=3))
-        ps_acc = ctx.enter_context(tc.psum_pool(name="ps_acc", bufs=1))
+        ps_tr = ctx.enter_context(tc.psum_pool(name="ps_tr", bufs=2))
+        ps_mx = ctx.enter_context(tc.psum_pool(name="ps_mx", bufs=1))
+        ps_cut = ctx.enter_context(tc.psum_pool(name="ps_cut", bufs=4))
+        ps_near = ctx.enter_context(tc.psum_pool(name="ps_near", bufs=1))
 
         ident = const.tile([P, P], F32, name="ident")
         make_identity(nc, ident[:])
-        perm = const.tile([P, P], F32, name="perm")
-        nc.vector.tensor_copy(out=perm[:].rearrange("p (a h e) -> p a h e", a=A, h=H),
-                              in_=ident[:].rearrange("p (h a e) -> p a h e", h=H, a=A))
-        pbuf = const.tile([P, A, P], F32, name="pbuf")
-        nc.vector.memset(pbuf[:], 0.0)
-
-        wc = const.tile([P, 2, 3 * P], U32, name="wc", align_bytes=64)
-        ws = const.tile([P, 2, 3 * P], U8, name="ws", align_bytes=64)
+        w_codes = const.tile([P, 2, 3 * P], U32, name="w_codes", align_bytes=64)
+        w_scales = const.tile([P, 2, 3 * P], U8, name="w_scales", align_bytes=64)
         bias_col = const.tile([P, 4], F32, name="bias_col")
         pb_bc = const.tile([P, H, NTAP], F32, name="pb_bc")
         g_raw = const.tile([P, B, H, NT, NS], BF16, name="g_raw")
-        sp = const.tile([P, H], F32, name="sp")
-        k_a = const.tile([P, NT, E], F32, name="k_a")
-        v_a = const.tile([P, VRING, E], F32, name="v_a")
-        v_b = const.tile([P, BRING, E], F32, name="v_b")
+        bypass = const.tile([P, H], F32, name="bypass")
+        k_tok = const.tile([P, NT, E], F32, name="k_tok")
+        v_tok = const.tile([P, VRING, E], F32, name="v_tok")
+        v_half = const.tile([P, BRING, E], F32, name="v_half")
         held = const.tile([P, (NCHUNK - HOLD0) * TPC, E], F32, name="held")
-        d_rows = [const.tile([P, H, 2, ROW], F32, name="d_rows%d" % i) for i in range(NSLOT)]
-        for d_t in d_rows:
-            nc.gpsimd.memset(d_t[:], 0.0)
-        junk = const.tile([P, HD], F32, name="junk")
+        spare = const.tile([P, HD], F32, name="spare")
+        rows = const.tile([P, H, TPC, ROW], F32, name="rows")
+        nc.gpsimd.memset(rows[:], 0.0)
 
         with tc.tile_pool(name="setup", bufs=1) as setup:
             w_sb = setup.tile([P, 3, D], BF16, name="w_sb")
@@ -100,26 +94,26 @@ def tile_dwarfattention_pa_t_kernel(tc, x, W_qkv, b_qkv, gains, pos_bias, identi
                 for h in range(H):
                     nc.scalar.dma_start(out=g_raw[:, b, h, :, :], in_=gains[b, h].rearrange("(t p) j -> p t j", p=P))
 
-            wg = setup.tile([P, 2, 3 * P, 2], F32, name="wg", align_bytes=64)
+            w_grouped = setup.tile([P, 2, 3 * P, 2], F32, name="w_grouped", align_bytes=64)
             for f in range(3):
-                wt = ps_xt.tile([P, 4, P], F32, name="wt", tag="xt")
-                ww = w_sb[:, f, :].bitcast(F32)
+                w_tr = ps_tr.tile([P, 4, P], F32, name="w_tr", tag="tr")
+                words = w_sb[:, f, :].bitcast(F32)
                 for j in range(4):
-                    nc.tensor.transpose(out=wt[:, j, :], in_=ww[:, j * P:(j + 1) * P], identity=ident[:])
-                nc.vector.tensor_copy(out=wg[:, :, f * P:(f + 1) * P, :],
-                                      in_=wt[:].rearrange("p (g u) r -> p g r u", u=2))
+                    nc.tensor.transpose(out=w_tr[:, j, :], in_=words[:, j * P:(j + 1) * P], identity=ident[:])
+                nc.vector.tensor_copy(out=w_grouped[:, :, f * P:(f + 1) * P, :],
+                                      in_=w_tr[:].rearrange("p (g u) r -> p g r u", u=2))
             for g in range(2):
                 for f in range(3):
                     nc.vector.quantize_mx(
-                        out=wc[:, g, f * P:(f + 1) * P].bitcast(FP8X4),
-                        scales=ws[:, g, f * P:(f + 1) * P],
-                        in_=wg[:, g, f * P:(f + 1) * P, :].rearrange("p r u -> p (r u)").bitcast(BF16))
+                        out=w_codes[:, g, f * P:(f + 1) * P].bitcast(FP8X4),
+                        scales=w_scales[:, g, f * P:(f + 1) * P],
+                        in_=w_grouped[:, g, f * P:(f + 1) * P, :].rearrange("p r u -> p (r u)").bitcast(BF16))
 
             b_rows32 = setup.tile([P, P], F32, name="b_rows32")
             nc.vector.tensor_copy(out=b_rows32[:], in_=b_rows[:])
-            bt = ps_xt.tile([P, 4, P], F32, name="bt", tag="xt")
-            nc.tensor.transpose(out=bt[:, 0, :], in_=b_rows32[:], identity=ident[:])
-            nc.vector.tensor_copy(out=bias_col[:, 0:3], in_=bt[:, 0, 0:3])
+            b_tr = ps_tr.tile([P, 4, P], F32, name="b_tr", tag="tr")
+            nc.tensor.transpose(out=b_tr[:, 0, :], in_=b_rows32[:], identity=ident[:])
+            nc.vector.tensor_copy(out=bias_col[:, 0:3], in_=b_tr[:, 0, 0:3])
 
             nc.vector.memset(pb_bc[:], 0.0)
             nc.vector.tensor_copy(out=pb_bc[:, :, 1:NTAP].rearrange("p h (t j) -> p h t j", t=4),
@@ -132,358 +126,274 @@ def tile_dwarfattention_pa_t_kernel(tc, x, W_qkv, b_qkv, gains, pos_bias, identi
             nc.scalar.activation(out=ib_e[:], in_=ib_e[:], func=ACTF.Exp, scale=-1.0)
             nc.vector.tensor_scalar_add(out=ib_e[:], in0=ib_e[:], scalar1=1.0)
             nc.scalar.activation(out=ib_e[:], in_=ib_e[:], func=ACTF.Ln)
-            nc.vector.scalar_tensor_tensor(out=sp[:], in0=ib[:], scalar=0.0, in1=ib_e[:], op0=ALU.max, op1=ALU.add)
+            nc.vector.scalar_tensor_tensor(out=bypass[:], in0=ib[:], scalar=0.0, in1=ib_e[:],
+                                           op0=ALU.max, op1=ALU.add)
 
+        x_pool = ctx.enter_context(tc.tile_pool(name="x_pool", bufs=2))
+        grouped_pool = ctx.enter_context(tc.tile_pool(name="grouped_pool", bufs=2))
+        code_pool = ctx.enter_context(tc.tile_pool(name="code_pool", bufs=2))
+        kf_pool = ctx.enter_context(tc.tile_pool(name="kf_pool", bufs=3))
+        vf_pool = ctx.enter_context(tc.tile_pool(name="vf_pool", bufs=3))
+        q_pool = ctx.enter_context(tc.tile_pool(name="q_pool", bufs=3))
+        prod_pool = ctx.enter_context(tc.tile_pool(name="prod_pool", bufs=3))
+        score_pool = ctx.enter_context(tc.tile_pool(name="score_pool", bufs=3))
+        tap_pool = ctx.enter_context(tc.tile_pool(name="tap_pool", bufs=3))
+        band_pool = ctx.enter_context(tc.tile_pool(name="band_pool", bufs=2))
+        out_pool = ctx.enter_context(tc.tile_pool(name="out_pool", bufs=2))
 
-        xp = ctx.enter_context(tc.tile_pool(name="xp", bufs=2))
-        gp = ctx.enter_context(tc.tile_pool(name="gp", bufs=2))
-        cp = ctx.enter_context(tc.tile_pool(name="cp", bufs=2))
-        kwp = ctx.enter_context(tc.tile_pool(name="kwp", bufs=3))
-        vwp = ctx.enter_context(tc.tile_pool(name="vwp", bufs=3))
-        ap_pool = ctx.enter_context(tc.tile_pool(name="ap_pool", bufs=2))
-        qp = ctx.enter_context(tc.tile_pool(name="qp", bufs=3))
-        pp = ctx.enter_context(tc.tile_pool(name="pp", bufs=2))
-        sp_pool = ctx.enter_context(tc.tile_pool(name="sp_pool", bufs=3))
-        cm = ctx.enter_context(tc.tile_pool(name="cm", bufs=3))
-        accp = ctx.enter_context(tc.tile_pool(name="accp", bufs=2))
-        stp = ctx.enter_context(tc.tile_pool(name="stp", bufs=2))
+        x_of, grouped_of, code_of = {}, {}, {}
+        kf_of, vf_of, q_of = {}, {}, {}
+        score_of, weight_of, skewed_of, band_of, o_of = {}, {}, {}, {}, {}
+        scratch = out.rearrange("b n e -> (b n e)")
 
-        kw = {}
-        vw = {}
-        q_of = {}
-        q2_of = {}
-        s_of = {}
+        def feature_major(c):
+            if c not in kf_of:
+                kf_of[c] = kf_pool.tile([P, KWIN + CH], F32, name="kf")
+                vf_of[c] = vf_pool.tile([P, VWIN + CH], F32, name="vf")
+            return kf_of[c], vf_of[c]
 
-        def window(c):
-            if c not in kw:
-                kw[c] = kwp.tile([P, WIN + CH], F32, name="kw")
-                vw[c] = vwp.tile([P, WINV + CH], F32, name="vw")
-            return kw[c], vw[c]
-
-        x_of = {}
-        grp_of = {}
-        code_of = {}
-
-        def fe_load(c):
+        def load_x(c):
             b, cc = divmod(c, NCC)
-            n0 = cc * CH
-            x_sb = xp.tile([P, TPC, D], BF16, name="x_sb")
-            nc.sync.dma_start(out=x_sb[:], in_=x[b, n0:n0 + CH, :].rearrange("(t p) k -> p t k", p=P))
-            x_of[c] = x_sb
+            x_of[c] = x_pool.tile([P, TPC, D], BF16, name="x_sb")
+            nc.sync.dma_start(out=x_of[c][:],
+                              in_=x[b, cc * CH:(cc + 1) * CH, :].rearrange("(t p) k -> p t k", p=P))
 
-        def fe_xpose(c, tl):
+        def transpose_x(c, tl):
             if tl == 0:
-                grp_of[c] = gp.tile([P, 2, CH, 2], F32, name="grp", align_bytes=64)
-            grp = grp_of[c]
-            xt = ps_xt.tile([P, 4, P], F32, name="xt", tag="xt")
-            xw = x_of[c][:, tl, :].bitcast(F32)
+                grouped_of[c] = grouped_pool.tile([P, 2, CH, 2], F32, name="grouped", align_bytes=64)
+            x_tr = ps_tr.tile([P, 4, P], F32, name="x_tr", tag="tr")
+            words = x_of[c][:, tl, :].bitcast(F32)
             for j in range(4):
-                nc.tensor.transpose(out=xt[:, j, :], in_=xw[:, j * P:(j + 1) * P], identity=ident[:])
-            nc.scalar.copy(out=grp[:, :, tl * P:(tl + 1) * P, :],
-                           in_=xt[:].rearrange("p (g u) r -> p g r u", u=2))
+                nc.tensor.transpose(out=x_tr[:, j, :], in_=words[:, j * P:(j + 1) * P], identity=ident[:])
+            nc.scalar.copy(out=grouped_of[c][:, :, tl * P:(tl + 1) * P, :],
+                           in_=x_tr[:].rearrange("p (g u) r -> p g r u", u=2))
 
-        def fe_quant(c):
-            grp = grp_of[c]
-            codes = cp.tile([P, 2, CH], U32, name="codes", align_bytes=64)
-            scl = cp.tile([P, 2, CH], U8, name="scl", align_bytes=64)
+        def quantise_x(c):
+            codes = code_pool.tile([P, 2, CH], U32, name="codes", align_bytes=64)
+            scales = code_pool.tile([P, 2, CH], U8, name="scales", align_bytes=64)
             for g in range(2):
-                nc.vector.quantize_mx(out=codes[:, g, :].bitcast(FP8X4), scales=scl[:, g, :],
-                                      in_=grp[:, g, :, :].rearrange("p r u -> p (r u)").bitcast(BF16))
-            code_of[c] = (codes, scl)
+                nc.vector.quantize_mx(
+                    out=codes[:, g, :].bitcast(FP8X4), scales=scales[:, g, :],
+                    in_=grouped_of[c][:, g, :, :].rearrange("p r u -> p (r u)").bitcast(BF16))
+            code_of[c] = (codes, scales)
 
-        def fe_kv(c):
-            b, cc = divmod(c, NCC)
-            codes, scl = code_of[c]
-            kwc, vwc = window(c)
-            if cc == 0:
-                nc.vector.memset(kwc[:, 0:WIN], 0.0)
-                nc.vector.memset(vwc[:, 0:WINV], 0.0)
-            for f, dst, win in ((1, kwc, WIN), (2, vwc, WINV)):
-                ps = ps_mm.tile([P, CH], F32, name="ps", tag="mm")
-                for g in range(2):
-                    nc.tensor.matmul_mx(out=ps[:], lhsT=wc[:, g, f * P:(f + 1) * P].bitcast(FP8X4),
-                                        lhsT_scale=ws[:, g, f * P:(f + 1) * P],
-                                        rhs=codes[:, g, :].bitcast(FP8X4), rhs_scale=scl[:, g, :],
-                                        start=(g == 0), stop=(g == 1))
-                nc.scalar.activation(out=dst[:, win:win + CH], in_=ps[:], func=ACTF.Identity,
-                                     bias=bias_col[:, f:f + 1], scale=1.0)
-                if cc + 1 < NCC:
-                    nxt = window(c + 1)[f - 1]
-                    nc.scalar.activation(out=nxt[:, 0:win], in_=ps[:, CH - win:CH], func=ACTF.Identity,
-                                         bias=bias_col[:, f:f + 1], scale=1.0)
-
-        def fe_q(c):
-            codes, scl = code_of[c]
-            psq = ps_mm.tile([P, CH], F32, name="psq", tag="mm")
+        def project(c, f):
+            codes, scales = code_of[c]
+            acc = ps_mx.tile([P, CH], F32, name="acc", tag="mx")
             for g in range(2):
-                nc.tensor.matmul_mx(out=psq[:], lhsT=wc[:, g, 0:P].bitcast(FP8X4), lhsT_scale=ws[:, g, 0:P],
-                                    rhs=codes[:, g, :].bitcast(FP8X4), rhs_scale=scl[:, g, :],
+                nc.tensor.matmul_mx(out=acc[:], lhsT=w_codes[:, g, f * P:(f + 1) * P].bitcast(FP8X4),
+                                    lhsT_scale=w_scales[:, g, f * P:(f + 1) * P],
+                                    rhs=codes[:, g, :].bitcast(FP8X4), rhs_scale=scales[:, g, :],
                                     start=(g == 0), stop=(g == 1))
-            q_t = qp.tile([P, CH], F32, name="q_t")
-            nc.scalar.activation(out=q_t[:], in_=psq[:], func=ACTF.Identity, bias=bias_col[:, 0:1], scale=1.0)
-            tq = ps_xt.tile([P, TPC, P], F32, name="tq", tag="xt")
-            for tl in range(TPC):
-                nc.tensor.transpose(out=tq[:, tl, :], in_=q_t[:, tl * P:(tl + 1) * P], identity=ident[:])
-            q_sb = qp.tile([P, TPC, E], F32, name="q_sb")
-            nc.scalar.copy(out=q_sb[:], in_=tq[:])
-            tq2 = ps_xt.tile([P, TPC, P], F32, name="tq2", tag="xt")
-            for tl in range(TPC):
-                nc.tensor.transpose(out=tq2[:, tl, :], in_=q_t[:, tl * P:(tl + 1) * P], identity=perm[:])
-            q2_sb = qp.tile([P, TPC, E], F32, name="q2_sb")
-            nc.scalar.copy(out=q2_sb[:], in_=tq2[:])
-            q2_of[c] = q2_sb
-            q_of[c] = q_sb
+            return acc
 
-        def fe_ka(c):
-            b, cc = divmod(c, NCC)
+        def add_bias(dst, acc, f):
+            nc.scalar.activation(out=dst, in_=acc, func=ACTF.Identity, bias=bias_col[:, f:f + 1], scale=1.0)
+
+        def project_kv(c):
+            cc = c % NCC
+            for f, win in ((1, KWIN), (2, VWIN)):
+                dst = feature_major(c)[f - 1]
+                if cc == 0:
+                    nc.vector.memset(dst[:, 0:win], 0.0)
+                acc = project(c, f)
+                add_bias(dst[:, win:win + CH], acc[:], f)
+                if cc + 1 < NCC:
+                    add_bias(feature_major(c + 1)[f - 1][:, 0:win], acc[:, CH - win:CH], f)
+
+        def token_major(src, first, dst):
+            tr = ps_tr.tile([P, TPC, P], F32, name="tok_tr", tag="tr")
+            for tl in range(TPC):
+                nc.tensor.transpose(out=tr[:, tl, :], in_=src[:, first + tl * P:first + (tl + 1) * P],
+                                    identity=ident[:])
+            nc.scalar.copy(out=dst, in_=tr[:])
+
+        def project_q(c):
+            q_f = q_pool.tile([P, CH], F32, name="q_f")
+            add_bias(q_f[:], project(c, 0)[:], 0)
+            q_of[c] = q_pool.tile([P, TPC, E], F32, name="q_tok")
+            token_major(q_f, 0, q_of[c][:])
+
+        def turn_kv(c):
+            cc = c % NCC
             g0 = c * TPC
-            for src, first, dst, at in ((kw[c], WIN, k_a, cc * TPC), (vw[c], WINV, v_a, g0 % VRING),
-                                        (vw[c], 0, v_b, g0 % BRING)):
-                ta = ps_xt.tile([P, TPC, P], F32, name="ta", tag="xt")
-                for tl in range(TPC):
-                    nc.tensor.transpose(out=ta[:, tl, :], in_=src[:, first + tl * P:first + (tl + 1) * P],
-                                        identity=ident[:])
-                nc.scalar.copy(out=dst[:, at:at + TPC, :], in_=ta[:])
-
-        def shifted_groups(nv):
-            una = [s for s in range(nv) if OFFS[s] % P != 0]
-            return [una[i:i + 4] for i in range(0, len(una), 4)]
+            token_major(kf_of[c], KWIN, k_tok[:, cc * TPC:(cc + 1) * TPC, :])
+            token_major(vf_of[c], VWIN, v_tok[:, g0 % VRING:g0 % VRING + TPC, :])
+            token_major(vf_of[c], 0, v_half[:, g0 % BRING:g0 % BRING + TPC, :])
 
         def scores(c, tl):
-            b, cc = divmod(c, NCC)
-            kwc = kw[c]
-            q_sb = q_of[c]
+            cc = c % NCC
             if tl == 0:
-                s_of[c] = sp_pool.tile([P, H, TPC, NOFF], F32, name="s_t")
+                s_all = score_pool.tile([P, H, TPC, NOFF], F32, name="s_all")
+                s_two = score_pool.tile([P, H, TPC, 2], F32, name="s_two")
+                score_of[c] = (s_all, s_two)
                 if n_valid(cc * TPC) < NOFF:
-                    nc.vector.memset(s_of[c][:], 0.0)
-            s_t = s_of[c]
+                    nc.vector.memset(s_all[:], 0.0)
+            s_all, s_two = score_of[c]
             t = cc * TPC + tl
             nv = n_valid(t)
-            s_out = s_t[:, :, tl, 0:nv].rearrange("p h s -> p s h")
-            if REDUCER[(c * TPC + tl) % len(REDUCER)] == "V":
-                prod = pp.tile([P, NOFF, E], F32, name="prod")
-                qb = q_sb[:, tl, :]
-                for grp_s in shifted_groups(nv):
-                    ko = ps_ko.tile([P, 4, P], F32, name="ko", tag="ko")
-                    for i, s in enumerate(grp_s):
-                        col = WIN + tl * P - OFFS[s]
-                        nc.tensor.transpose(out=ko[:, i, :], in_=kwc[:, col:col + P], identity=ident[:])
-                    for i0, s0, ln in runs_of(list(enumerate(grp_s))):
-                        nc.vector.tensor_tensor(out=prod[:, s0:s0 + ln, :], in0=ko[:, i0:i0 + ln, :],
-                                                in1=qb.unsqueeze(1).to_broadcast([P, ln, E]), op=ALU.mult)
-                for s in range(nv):
-                    if OFFS[s] % P == 0:
-                        nc.vector.tensor_tensor(out=prod[:, s, :], in0=k_a[:, t - OFFS[s] // P, :],
-                                                in1=qb, op=ALU.mult)
-                nc.vector.tensor_reduce(out=s_out, in_=prod[:, 0:nv, :].rearrange("p s (h d) -> p s h d", h=H),
-                                        axis=AX.X, op=ALU.add)
-            else:
-                q2 = q2_of[c][:, tl, :].rearrange("p (a k) -> p a k", k=4)
-                for grp_s in shifted_groups(nv):
-                    ko = ps_ko.tile([P, 4, P], F32, name="ko", tag="ko")
-                    for i, s in enumerate(grp_s):
-                        col = WIN + tl * P - OFFS[s]
-                        nc.tensor.transpose(out=ko[:, i, :], in_=kwc[:, col:col + P], identity=perm[:])
-                    for i0, s0, ln in runs_of(list(enumerate(grp_s))):
-                        nc.vector.tensor_tensor(
-                            out=pbuf[:, :, 4 * s0:4 * (s0 + ln)].rearrange("p a (s k) -> p a s k", k=4),
-                            in0=ko[:, i0:i0 + ln, :].rearrange("p s (a k) -> p a s k", k=4),
-                            in1=q2.unsqueeze(2).to_broadcast([P, A, ln, 4]), op=ALU.mult)
-                for s in range(nv):
-                    if OFFS[s] % P == 0:
-                        nc.vector.tensor_tensor(
-                            out=pbuf[:, :, 4 * s:4 * s + 4].rearrange("p a (h e) -> p a h e", h=H),
-                            in0=k_a[:, t - OFFS[s] // P, :].rearrange("p (h a e) -> p a h e", h=H, a=A),
-                            in1=q2.rearrange("p a (h e) -> p a h e", h=H), op=ALU.mult)
-                st = ps_st.tile([P, P], F32, name="st", tag="st")
-                for a in range(A):
-                    nc.tensor.matmul(out=st[:], lhsT=pbuf[:, a, :], rhs=ident[:], is_transpose=True,
-                                     start=(a == 0), stop=(a == A - 1))
-                st_sb = stp.tile([P, P], F32, name="st_sb")
-                nc.scalar.copy(out=st_sb[:], in_=st[:])
-                bk = ps_st.tile([P, P], F32, name="bk", tag="st")
-                nc.tensor.transpose(out=bk[:], in_=st_sb[:], identity=ident[:])
-                nc.vector.tensor_reduce(out=s_out, in_=bk[:, 0:4 * nv].rearrange("p (s h e) -> p s h e", h=H, e=2),
-                                        axis=AX.X, op=ALU.add)
+            q_t = q_of[c][:, tl, :]
+            prod = prod_pool.tile([P, NOFF, E], F32, name="prod")
+            for places in cut_groups(nv):
+                cut = ps_cut.tile([P, 4, P], F32, name="cut", tag="cut")
+                for i, s in enumerate(places):
+                    first = KWIN + tl * P - OFFS[s]
+                    nc.tensor.transpose(out=cut[:, i, :], in_=kf_of[c][:, first:first + P], identity=ident[:])
+                for i0, s0, ln in runs_of(places):
+                    nc.vector.tensor_tensor(out=prod[:, s0:s0 + ln, :], in0=cut[:, i0:i0 + ln, :],
+                                            in1=q_t.unsqueeze(1).to_broadcast([P, ln, E]), op=ALU.mult)
+            for s in range(nv):
+                if OFFS[s] % P == 0:
+                    nc.vector.tensor_tensor(out=prod[:, s, :], in0=k_tok[:, t - OFFS[s] // P, :], in1=q_t,
+                                            op=ALU.mult)
+            for s in range(2):
+                for h in range(H):
+                    nc.scalar.activation(out=spare[:], in_=prod[:, s, h * HD:(h + 1) * HD], func=ACTF.Copy,
+                                         accum_out=s_two[:, h, tl, s:s + 1])
+            nc.vector.tensor_reduce(out=s_all[:, :, tl, 2:nv].rearrange("p h s -> p s h"),
+                                    in_=prod[:, 2:nv, :].rearrange("p s (h d) -> p s h d", h=H),
+                                    axis=AX.X, op=ALU.add)
 
         def weights(c):
             b, cc = divmod(c, NCC)
-            s_t = s_of[c]
-            shp = [P, H, TPC, NTAP]
-            u = cm.tile(shp, F32, name="u")
-            spair = s_t[:, :, :, 2:NOFF].rearrange("p h t (i two) -> p h t i two", two=2)
-
-            nc.scalar.copy(out=u[:, :, :, 0:12], in_=s_t[:, :, :, 0:1].to_broadcast([P, H, TPC, 12]))
-            nc.scalar.copy(out=u[:, :, :, 12:13], in_=s_t[:, :, :, 1:2])
-            nc.scalar.copy(out=u[:, :, :, 13:23], in_=spair[:, :, :, 0:10, 0])
-            nc.scalar.copy(out=u[:, :, :, 23:34], in_=spair[:, :, :, 0:11, 0])
-            nc.scalar.copy(out=u[:, :, :, 34:45], in_=spair[:, :, :, 0:11, 1])
-            nc.vector.tensor_tensor(out=u[:], in0=u[:], in1=pb_bc[:].unsqueeze(2).to_broadcast(shp), op=ALU.add)
-            e = cm.tile(shp, F32, name="e")
-            nc.scalar.activation(out=e[:], in_=u[:], func=ACTF.Exp)
+            s_all, s_two = score_of[c]
+            shape = [P, H, TPC, NTAP]
+            pairs = s_all[:, :, :, 2:NOFF].rearrange("p h t (i two) -> p h t i two", two=2)
+            u = tap_pool.tile(shape, F32, name="u")
+            nc.scalar.copy(out=u[:, :, :, 0:12], in_=s_two[:, :, :, 0:1].to_broadcast([P, H, TPC, 12]))
+            nc.scalar.copy(out=u[:, :, :, 12:13], in_=s_two[:, :, :, 1:2])
+            nc.scalar.copy(out=u[:, :, :, 13:23], in_=pairs[:, :, :, 0:10, 0])
+            nc.scalar.copy(out=u[:, :, :, 23:34], in_=pairs[:, :, :, 0:11, 0])
+            nc.scalar.copy(out=u[:, :, :, 34:45], in_=pairs[:, :, :, 0:11, 1])
+            nc.vector.tensor_tensor(out=u[:], in0=u[:], in1=pb_bc[:].unsqueeze(2).to_broadcast(shape), op=ALU.add)
+            f = tap_pool.tile(shape, F32, name="f")
+            nc.scalar.activation(out=f[:], in_=u[:], func=ACTF.Exp)
             nc.scalar.activation(out=u[:], in_=u[:], func=ACTF.Relu)
-            nc.vector.scalar_tensor_tensor(out=e[:].rearrange("p h t k -> p (h t k)"),
-                                           in0=e[:].rearrange("p h t k -> p (h t k)"), scalar=1.0,
+            nc.vector.scalar_tensor_tensor(out=f[:].rearrange("p h t k -> p (h t k)"),
+                                           in0=f[:].rearrange("p h t k -> p (h t k)"), scalar=1.0,
                                            in1=u[:].rearrange("p h t k -> p (h t k)"), op0=ALU.min, op1=ALU.add)
-            gcc = cm.tile(shp, F32, name="gcc")
+            gain = tap_pool.tile(shape, F32, name="gain")
             for tau in range(4):
-                nc.scalar.activation(out=gcc[:, :, :, 1 + NS * tau:1 + NS * (tau + 1)],
+                nc.scalar.activation(out=gain[:, :, :, 1 + NS * tau:1 + NS * (tau + 1)],
                                      in_=g_raw[:, b, :, cc * TPC:(cc + 1) * TPC, :], func=ACTF.Copy, scale=D4[tau])
-            nc.scalar.copy(out=gcc[:, :, :, 0:1], in_=sp[:].unsqueeze(2).unsqueeze(3).to_broadcast([P, H, TPC, 1]))
-            wt = cm.tile(shp, F32, name="wt")
-            nc.vector.tensor_tensor(out=wt[:], in0=e[:], in1=gcc[:], op=ALU.mult)
-            z1 = cm.tile([P, H, TPC], F32, name="z1")
-            z3 = cm.tile([P, H, TPC], F32, name="z3")
-            nc.vector.tensor_reduce(out=z1[:], in_=wt[:], axis=AX.X, op=ALU.add)
-            nc.vector.tensor_reduce(out=z3[:], in_=wt[:, :, :, 34:45], axis=AX.X, op=ALU.add)
-            nc.vector.scalar_tensor_tensor(out=z1[:], in0=z3[:], scalar=-2.0, in1=z1[:], op0=ALU.mult, op1=ALU.add)
-            nc.vector.tensor_scalar_add(out=z1[:], in0=z1[:], scalar1=1e-6)
-            nc.vector.reciprocal(out=z3[:], in_=z1[:])
-            wn = wt
-            w0 = cm.tile([P, H, TPC], F32, name="w0")
-            nc.vector.tensor_reduce(out=w0[:], in_=wn[:, :, :, 0:12], axis=AX.X, op=ALU.add)
-            wp = cm.tile([P, H, TPC, 10], F32, name="wp")
-            nc.vector.tensor_tensor(out=wp[:], in0=wn[:, :, :, 13:23], in1=wn[:, :, :, 23:33], op=ALU.add)
+            nc.scalar.copy(out=gain[:, :, :, 0:1],
+                           in_=bypass[:].unsqueeze(2).unsqueeze(3).to_broadcast([P, H, TPC, 1]))
+            w_tap = tap_pool.tile(shape, F32, name="w_tap")
+            nc.vector.tensor_tensor(out=w_tap[:], in0=f[:], in1=gain[:], op=ALU.mult)
+            z = tap_pool.tile([P, H, TPC], F32, name="z")
+            rz = tap_pool.tile([P, H, TPC], F32, name="rz")
+            nc.vector.tensor_reduce(out=z[:], in_=w_tap[:], axis=AX.X, op=ALU.add)
+            nc.vector.tensor_reduce(out=rz[:], in_=w_tap[:, :, :, 34:45], axis=AX.X, op=ALU.add)
+            nc.vector.scalar_tensor_tensor(out=z[:], in0=rz[:], scalar=-2.0, in1=z[:], op0=ALU.mult, op1=ALU.add)
+            nc.vector.tensor_scalar_add(out=z[:], in0=z[:], scalar1=1e-6)
+            nc.vector.reciprocal(out=rz[:], in_=z[:])
+            w_zero = tap_pool.tile([P, H, TPC], F32, name="w_zero")
+            nc.vector.tensor_reduce(out=w_zero[:], in_=w_tap[:, :, :, 0:12], axis=AX.X, op=ALU.add)
+            w_pow = tap_pool.tile([P, H, TPC, 10], F32, name="w_pow")
+            nc.vector.tensor_tensor(out=w_pow[:], in0=w_tap[:, :, :, 13:23], in1=w_tap[:, :, :, 23:33], op=ALU.add)
 
-            def place(s):
+            def of_place(s):
                 if s == 0:
-                    return w0, None
+                    return w_zero[:]
                 if s == 1:
-                    return wn, 12
-                if s % 2 == 0:
-                    if s // 2 <= 10:
-                        return wp, s // 2 - 1
-                    return wn, 33
-                return wn, 34 + (s - 3) // 2
+                    return w_tap[:, :, :, 12]
+                if s % 2 == 1:
+                    return w_tap[:, :, :, 34 + (s - 3) // 2]
+                if s == NOFF - 2:
+                    return w_tap[:, :, :, 33]
+                return w_pow[:, :, :, s // 2 - 1]
 
-            def col(s, h, tl):
-                src, k = place(s)
-                if k is None:
-                    return src[:, h, tl:tl + 1]
-                return src[:, h, tl, k:k + 1]
+            weight_of[c] = (of_place, rz)
 
-            def cols(s, tl0):
-                src, k = place(s)
-                if k is None:
-                    return src[:, :, tl0:tl0 + 2]
-                return src[:, :, tl0:tl0 + 2, k]
-
-            return col, cols, z3
-
-        col_of = {}
-        a_of = {}
-        at_of = {}
-        o_of = {}
-        scr = out.rearrange("b n e -> (b n e)")
-
-        def skew(c, hc):
-            cols = col_of[c][1]
-            slot = (2 * c + hc) % NSLOT
-            d_t = d_rows[slot]
+        def skew(c):
+            of_place = weight_of[c][0]
             for s in range(NEAR):
-                nc.scalar.copy(out=d_t[:, :, :, P - OFFS[s]], in_=cols(s, 2 * hc))
-            area = scr[SCR0 + slot * 4 * UNIT:SCR0 + (slot + 1) * 4 * UNIT]
-            nc.sync.dma_start(out=area.rearrange("(u p w) -> p u w", u=4, p=P),
-                              in_=d_t[:].rearrange("p h t w -> p (h t) w"))
-            a_t = ap_pool.tile([P, 4, 2 * P], F32, name="a_t")
-            nc.sync.dma_start(out=a_t[:], in_=area.rearrange("(u r) -> u r", u=4)[:, 0:2 * P * P]
-                              .rearrange("u (p m) -> p u m", p=P))
-            a_of[(c, hc)] = a_t
+                nc.scalar.copy(out=rows[:, :, :, P - OFFS[s]], in_=of_place(s))
+            for h in range(H):
+                area = scratch[SCR0 + h * TPC * UNIT:SCR0 + (h + 1) * TPC * UNIT]
+                nc.sync.dma_start(out=area.rearrange("(t p w) -> p t w", t=TPC, p=P), in_=rows[:, h, :, :])
+                skewed_of[(c, h)] = band_pool.tile([P, TPC, 2 * P], F32, name="skewed")
+                nc.sync.dma_start(out=skewed_of[(c, h)][:],
+                                  in_=area.rearrange("(t r) -> t r", t=TPC)[:, 0:2 * P * P]
+                                  .rearrange("t (p m) -> p t m", p=P))
 
-        def prep(c, hc):
-            a_t = a_of[(c, hc)]
-            at_t = ap_pool.tile([P, 8, P], F32, name="at_t")
+        def band(c, h):
+            band_of[(c, h)] = band_pool.tile([P, 2 * TPC, P], F32, name="band")
             for half in range(2):
-                tp = ps_xt.tile([P, 4, P], F32, name="tp", tag="xt")
+                tr = ps_tr.tile([P, 4, P], F32, name="band_tr", tag="tr")
                 for i in range(4):
-                    u, kb = divmod(4 * half + i, 2)
-                    nc.tensor.transpose(out=tp[:, i, :], in_=a_t[:, u, kb * P:(kb + 1) * P], identity=ident[:])
-                nc.scalar.copy(out=at_t[:, 4 * half:4 * half + 4, :], in_=tp[:])
-            at_of[(c, hc)] = at_t
+                    tl, kb = divmod(4 * half + i, 2)
+                    nc.tensor.transpose(out=tr[:, i, :], in_=skewed_of[(c, h)][:, tl, kb * P:(kb + 1) * P],
+                                        identity=ident[:])
+                nc.scalar.copy(out=band_of[(c, h)][:, 4 * half:4 * half + 4, :], in_=tr[:])
 
-        def av(c, hc):
+        def values(c, h):
             b, cc = divmod(c, NCC)
-            col = col_of[c][0]
-            at_t = at_of[(c, hc)]
-            if hc == 0:
+            of_place, rz = weight_of[c]
+            hs = slice(h * HD, (h + 1) * HD)
+            if h == 0:
                 if c >= HOLD0:
                     o_of[c] = held[:, (c - HOLD0) * TPC:(c - HOLD0 + 1) * TPC, :]
                 else:
-                    o_of[c] = accp.tile([P, TPC, E], F32, name="o_sb")
+                    o_of[c] = out_pool.tile([P, TPC, E], F32, name="o_sb")
             o_sb = o_of[c]
-            near = ps_acc.tile([P, 4, HD], F32, name="near")
-            for h in range(H):
-                for t2 in range(2):
-                    u = 2 * h + t2
-                    t = cc * TPC + 2 * hc + t2
-                    g = c * TPC + 2 * hc + t2
-                    kbs = [kb for kb in range(2) if t - 1 + kb >= 0]
-                    for kb in kbs:
-                        nc.tensor.matmul(out=near[:, u, :], lhsT=at_t[:, 2 * u + kb, :],
-                                         rhs=v_a[:, (g - 1 + kb) % VRING, h * HD:(h + 1) * HD],
-                                         start=(kb == kbs[0]), stop=(kb == kbs[-1]))
-            for k in range(NEAR, NOFF + 1):
-                for t2 in range(2):
-                    tl = 2 * hc + t2
-                    t = cc * TPC + tl
+            near = ps_near.tile([P, TPC, HD], F32, name="near")
+            for tl in range(TPC):
+                blocks = [kb for kb in range(2) if cc * TPC + tl - 1 + kb >= 0]
+                for kb in blocks:
+                    nc.tensor.matmul(out=near[:, tl, :], lhsT=band_of[(c, h)][:, 2 * tl + kb, :],
+                                     rhs=v_tok[:, (c * TPC + tl - 1 + kb) % VRING, hs],
+                                     start=(kb == blocks[0]), stop=(kb == 1))
+            total = [near[:, tl, :] for tl in range(TPC)]
+            for s in range(NEAR, NOFF):
+                for tl in range(TPC):
                     g = c * TPC + tl
-                    nv = n_valid(t)
-                    for h in range(H):
-                        hs = slice(h * HD, (h + 1) * HD)
-                        prev = near[:, 2 * h + t2, :] if k == NEAR else o_sb[:, tl, hs]
-                        if k < nv:
-                            if OFFS[k] % P == 0:
-                                src = v_a[:, (g - OFFS[k] // P) % VRING, hs]
-                            else:
-                                src = v_b[:, (g - 1) % BRING, hs]
-                            nc.vector.scalar_tensor_tensor(out=o_sb[:, tl, hs], in0=src, scalar=col(k, h, tl),
-                                                           in1=prev, op0=ALU.mult, op1=ALU.add)
-                        elif k == NEAR:
-                            nc.vector.tensor_copy(out=o_sb[:, tl, hs], in_=prev)
-            rz = col_of[c][2]
-            for t2 in range(2):
-                tl = 2 * hc + t2
-                for h in range(H):
-                    hs = slice(h * HD, (h + 1) * HD)
-                    nc.scalar.activation(out=o_sb[:, tl, hs], in_=o_sb[:, tl, hs], func=ACTF.Copy,
-                                         scale=rz[:, h, tl:tl + 1])
-            if hc == 1 and c < HOLD0:
-                n0 = cc * CH
-                nc.sync.dma_start(out=out[b, n0:n0 + CH, :].rearrange("(t p) e -> p t e", p=P), in_=o_sb[:])
+                    if s < n_valid(cc * TPC + tl):
+                        if OFFS[s] % P == 0:
+                            shifted = v_tok[:, (g - OFFS[s] // P) % VRING, hs]
+                        else:
+                            shifted = v_half[:, (g - 1) % BRING, hs]
+                        nc.vector.scalar_tensor_tensor(out=o_sb[:, tl, hs], in0=shifted,
+                                                       scalar=of_place(s)[:, h, tl:tl + 1], in1=total[tl],
+                                                       op0=ALU.mult, op1=ALU.add)
+                        total[tl] = o_sb[:, tl, hs]
+            for tl in range(TPC):
+                nc.scalar.activation(out=o_sb[:, tl, hs], in_=total[tl], func=ACTF.Copy, scale=rz[:, h, tl:tl + 1])
+            if h == H - 1 and c < HOLD0:
+                nc.sync.dma_start(out=out[b, cc * CH:(cc + 1) * CH, :].rearrange("(t p) e -> p t e", p=P),
+                                  in_=o_sb[:])
 
-        def ok(c):
+        def is_chunk(c):
             return 0 <= c < NCHUNK
 
-        fe_load(0)
-        fe_load(1)
+        load_x(0)
+        load_x(1)
         for c in range(-2, NCHUNK + 3):
             for tl in range(TPC):
-                if tl == 0 and ok(c + 3) and c + 3 >= 2:
-                    fe_load(c + 3)
-                if ok(c + 2):
-                    fe_xpose(c + 2, tl)
-                if ok(c + 1):
+                if tl == 0 and is_chunk(c + 3) and c + 3 >= 2:
+                    load_x(c + 3)
+                if is_chunk(c + 2):
+                    transpose_x(c + 2, tl)
+                if is_chunk(c + 1):
                     if tl == 0:
-                        fe_quant(c + 1)
+                        quantise_x(c + 1)
                     if tl == 1:
-                        fe_kv(c + 1)
+                        project_kv(c + 1)
                     if tl == 2:
-                        fe_q(c + 1)
-                        fe_ka(c + 1)
-                if ok(c):
+                        project_q(c + 1)
+                        turn_kv(c + 1)
+                if is_chunk(c):
                     scores(c, tl)
-                if tl == 1 and ok(c - 1):
-                    col_of[c - 1] = weights(c - 1)
-                    skew(c - 1, 0)
-                    skew(c - 1, 1)
-                if tl == 3 and ok(c - 1):
-                    prep(c - 1, 0)
-                if tl == 0 and ok(c - 2):
-                    prep(c - 2, 1)
-                    av(c - 2, 0)
-                if tl == 1 and ok(c - 2):
-                    av(c - 2, 1)
+                if tl == 1 and is_chunk(c - 1):
+                    weights(c - 1)
+                    skew(c - 1)
+                if tl == 3 and is_chunk(c - 1):
+                    band(c - 1, 0)
+                if tl == 0 and is_chunk(c - 2):
+                    band(c - 2, 1)
+                    values(c - 2, 0)
+                if tl == 1 and is_chunk(c - 2):
+                    values(c - 2, 1)
         for c in range(HOLD0, NCHUNK):
             b, cc = divmod(c, NCC)
             nc.sync.dma_start(out=out[b, cc * CH:(cc + 1) * CH, :].rearrange("(t p) e -> p t e", p=P),

@@ -25,6 +25,7 @@ OFFS = tuple(sorted([0] + [1 << i for i in range(12)] + [3 << j for j in range(1
 NOFF = len(OFFS)
 NTAP = 1 + 4 * NS
 NEAR = 15
+NFEW = 4
 KWIN = 256
 VWIN = 64
 ROW = 2 * P + 1
@@ -225,11 +226,11 @@ def tile_dwarfattention_pa_t_kernel(tc, x, W_qkv, b_qkv, gains, pos_bias, identi
             cc = c % NCC
             if tl == 0:
                 s_all = score_pool.tile([P, H, TPC, NOFF], F32, name="s_all")
-                s_two = score_pool.tile([P, H, TPC, 2], F32, name="s_two")
-                score_of[c] = (s_all, s_two)
+                s_few = score_pool.tile([P, H, TPC, NFEW], F32, name="s_few")
+                score_of[c] = (s_all, s_few)
                 if n_valid(cc * TPC) < NOFF:
                     nc.vector.memset(s_all[:], 0.0)
-            s_all, s_two = score_of[c]
+            s_all, s_few = score_of[c]
             t = cc * TPC + tl
             nv = n_valid(t)
             q_t = q_of[c][:, tl, :]
@@ -246,25 +247,27 @@ def tile_dwarfattention_pa_t_kernel(tc, x, W_qkv, b_qkv, gains, pos_bias, identi
                 if OFFS[s] % P == 0:
                     nc.vector.tensor_tensor(out=prod[:, s, :], in0=k_tok[:, t - OFFS[s] // P, :], in1=q_t,
                                             op=ALU.mult)
-            for s in range(2):
+            for s in range(NFEW):
                 for h in range(H):
                     nc.scalar.activation(out=spare[:], in_=prod[:, s, h * HD:(h + 1) * HD], func=ACTF.Copy,
-                                         accum_out=s_two[:, h, tl, s:s + 1])
-            nc.vector.tensor_reduce(out=s_all[:, :, tl, 2:nv].rearrange("p h s -> p s h"),
-                                    in_=prod[:, 2:nv, :].rearrange("p s (h d) -> p s h d", h=H),
+                                         accum_out=s_few[:, h, tl, s:s + 1])
+            nc.vector.tensor_reduce(out=s_all[:, :, tl, NFEW:nv].rearrange("p h s -> p s h"),
+                                    in_=prod[:, NFEW:nv, :].rearrange("p s (h d) -> p s h d", h=H),
                                     axis=AX.X, op=ALU.add)
 
         def weights(c):
             b, cc = divmod(c, NCC)
-            s_all, s_two = score_of[c]
+            s_all, s_few = score_of[c]
             shape = [P, H, TPC, NTAP]
-            pairs = s_all[:, :, :, 2:NOFF].rearrange("p h t (i two) -> p h t i two", two=2)
+            pairs = s_all[:, :, :, NFEW:NOFF].rearrange("p h t (i two) -> p h t i two", two=2)
             u = tap_pool.tile(shape, F32, name="u")
-            nc.scalar.copy(out=u[:, :, :, 0:12], in_=s_two[:, :, :, 0:1].to_broadcast([P, H, TPC, 12]))
-            nc.scalar.copy(out=u[:, :, :, 12:13], in_=s_two[:, :, :, 1:2])
-            nc.scalar.copy(out=u[:, :, :, 13:23], in_=pairs[:, :, :, 0:10, 0])
-            nc.scalar.copy(out=u[:, :, :, 23:34], in_=pairs[:, :, :, 0:11, 0])
-            nc.scalar.copy(out=u[:, :, :, 34:45], in_=pairs[:, :, :, 0:11, 1])
+            nc.scalar.copy(out=u[:, :, :, 0:12], in_=s_few[:, :, :, 0:1].to_broadcast([P, H, TPC, 12]))
+            nc.scalar.copy(out=u[:, :, :, 12:14], in_=s_few[:, :, :, 1:3])
+            nc.scalar.copy(out=u[:, :, :, 14:23], in_=pairs[:, :, :, 0:9, 0])
+            nc.scalar.copy(out=u[:, :, :, 23:24], in_=s_few[:, :, :, 2:3])
+            nc.scalar.copy(out=u[:, :, :, 24:34], in_=pairs[:, :, :, 0:10, 0])
+            nc.scalar.copy(out=u[:, :, :, 34:35], in_=s_few[:, :, :, 3:4])
+            nc.scalar.copy(out=u[:, :, :, 35:45], in_=pairs[:, :, :, 0:10, 1])
             nc.vector.tensor_tensor(out=u[:], in0=u[:], in1=pb_bc[:].unsqueeze(2).to_broadcast(shape), op=ALU.add)
             f = tap_pool.tile(shape, F32, name="f")
             nc.scalar.activation(out=f[:], in_=u[:], func=ACTF.Exp)

@@ -25,7 +25,7 @@ OFFS = tuple(sorted([0] + [1 << i for i in range(12)] + [3 << j for j in range(1
 NOFF = len(OFFS)
 NTAP = 1 + 4 * NS
 NEAR = 15
-NFEW = 4
+NFEW = 6
 KWIN = 256
 VWIN = 64
 ROW = 2 * P + 1
@@ -259,15 +259,18 @@ def tile_dwarfattention_pa_t_kernel(tc, x, W_qkv, b_qkv, gains, pos_bias, identi
             b, cc = divmod(c, NCC)
             s_all, s_few = score_of[c]
             shape = [P, H, TPC, NTAP]
+            nf = (NFEW - 2) // 2
+            few = s_few[:, :, :, 2:NFEW].rearrange("p h t (i two) -> p h t i two", two=2)
             pairs = s_all[:, :, :, NFEW:NOFF].rearrange("p h t (i two) -> p h t i two", two=2)
             u = tap_pool.tile(shape, F32, name="u")
             nc.scalar.copy(out=u[:, :, :, 0:12], in_=s_few[:, :, :, 0:1].to_broadcast([P, H, TPC, 12]))
-            nc.scalar.copy(out=u[:, :, :, 12:14], in_=s_few[:, :, :, 1:3])
-            nc.scalar.copy(out=u[:, :, :, 14:23], in_=pairs[:, :, :, 0:9, 0])
-            nc.scalar.copy(out=u[:, :, :, 23:24], in_=s_few[:, :, :, 2:3])
-            nc.scalar.copy(out=u[:, :, :, 24:34], in_=pairs[:, :, :, 0:10, 0])
-            nc.scalar.copy(out=u[:, :, :, 34:35], in_=s_few[:, :, :, 3:4])
-            nc.scalar.copy(out=u[:, :, :, 35:45], in_=pairs[:, :, :, 0:10, 1])
+            nc.scalar.copy(out=u[:, :, :, 12:13], in_=s_few[:, :, :, 1:2])
+            nc.scalar.copy(out=u[:, :, :, 13:13 + nf], in_=few[:, :, :, :, 0])
+            nc.scalar.copy(out=u[:, :, :, 13 + nf:23], in_=pairs[:, :, :, 0:10 - nf, 0])
+            nc.scalar.copy(out=u[:, :, :, 23:23 + nf], in_=few[:, :, :, :, 0])
+            nc.scalar.copy(out=u[:, :, :, 23 + nf:34], in_=pairs[:, :, :, 0:11 - nf, 0])
+            nc.scalar.copy(out=u[:, :, :, 34:34 + nf], in_=few[:, :, :, :, 1])
+            nc.scalar.copy(out=u[:, :, :, 34 + nf:45], in_=pairs[:, :, :, 0:11 - nf, 1])
             nc.vector.tensor_tensor(out=u[:], in0=u[:], in1=pb_bc[:].unsqueeze(2).to_broadcast(shape), op=ALU.add)
             f = tap_pool.tile(shape, F32, name="f")
             nc.scalar.activation(out=f[:], in_=u[:], func=ACTF.Exp)

from contextlib import ExitStack

import concourse.mybir as mybir
from concourse.masks import make_identity

F32 = mybir.dt.float32
BF16 = mybir.dt.bfloat16
U32 = mybir.dt.uint32
U8 = mybir.dt.uint8
FP8X4 = mybir.dt.float8_e4m3fn_x4
ALU = mybir.AluOpType
ACTF = mybir.ActivationFunctionType
AX = mybir.AxisListType

P = 128
B, N, D, H, HD, NS = 2, 4096, 1024, 2, 64, 11
E = H * HD
CH = 512
TPC = CH // P
NCC = N // CH
NT = N // P
NCHUNK = B * NCC
D4 = (0.4829629131445341, 0.8365163037378079, 0.2241438680420134, -0.1294095225512604)
OFFS = tuple(sorted([0] + [1 << i for i in range(12)] + [3 << j for j in range(11)]))
NOFF = len(OFFS)
NTAP = 1 + 4 * NS
NEAR = 15
NFEW = 6
KWIN = 256
VWIN = 64
ROW = 2 * P + 1
UNIT = P * ROW
VRING = 48
BRING = 16
SCR0 = B * N * E - H * TPC * UNIT
HOLD0 = SCR0 // (CH * E)
FLOPS = 2 * B * N * D * 3 * E + 4 * B * H * N * HD * NOFF


def n_valid(t):
    return len([o for o in OFFS if o <= t * P + P - 1])


def cut_groups(nv):
    cut = [s for s in range(nv) if OFFS[s] % P != 0]
    return [cut[i:i + 4] for i in range(0, len(cut), 4)]


def runs_of(places):
    runs = []
    for i, s in enumerate(places):
        if runs and runs[-1][1] + runs[-1][2] == s:
            runs[-1][2] += 1
        else:
            runs.append([i, s, 1])
    return runs


def tile_dwarfattention_pa_t_kernel(tc, x, W_qkv, b_qkv, gains, pos_bias, identity_bypass, out):
    nc = tc.nc
    with ExitStack() as ctx:
        const = ctx.enter_context(tc.tile_pool(name="const", bufs=1))
        ps_tr = ctx.enter_context(tc.psum_pool(name="ps_tr", bufs=2))
        ps_mx = ctx.enter_context(tc.psum_pool(name="ps_mx", bufs=1))
        ps_cut = ctx.enter_context(tc.psum_pool(name="ps_cut", bufs=4))
        ps_near = ctx.enter_context(tc.psum_pool(name="ps_near", bufs=1))

        ident = const.tile([P, P], F32, name="ident")
        make_identity(nc, ident[:])
        w_codes = const.tile([P, 2, 3 * P], U32, name="w_codes", align_bytes=64)
        w_scales = const.tile([P, 2, 3 * P], U8, name="w_scales", align_bytes=64)
        bias_col = const.tile([P, 4], F32, name="bias_col")
        pb_bc = const.tile([P, H, NTAP], F32, name="pb_bc")
        g_raw = const.tile([P, B, H, NT, NS], BF16, name="g_raw")
        bypass = const.tile([P, H], F32, name="bypass")
        k_tok = const.tile([P, NT, E], F32, name="k_tok")
        v_tok = const.tile([P, VRING, E], F32, name="v_tok")
        v_half = const.tile([P, BRING, E], F32, name="v_half")
        held = const.tile([P, (NCHUNK - HOLD0) * TPC, E], F32, name="held")
        spare = const.tile([P, HD], F32, name="spare")
        rows = const.tile([P, H, TPC, ROW], F32, name="rows")
        nc.gpsimd.memset(rows[:], 0.0)

        with tc.tile_pool(name="setup", bufs=1) as setup:
            w_sb = setup.tile([P, 3, D], BF16, name="w_sb")
            nc.sync.dma_start(out=w_sb[:], in_=W_qkv.rearrange("(f p) k -> p f k", p=P))
            b_rows = setup.tile([P, P], BF16, name="b_rows")
            nc.vector.memset(b_rows[:], 0.0)
            nc.scalar.dma_start(out=b_rows[0:3, :], in_=b_qkv.rearrange("(f c) -> f c", c=P))
            pb_raw = setup.tile([P, 4 * NS * H], BF16, name="pb_raw")
            nc.scalar.dma_start(out=pb_raw[:], in_=pos_bias.rearrange("r h -> (r h)").partition_broadcast(P))
            ib_raw = setup.tile([P, H], BF16, name="ib_raw")
            nc.scalar.dma_start(out=ib_raw[:], in_=identity_bypass.partition_broadcast(P))
            for b in range(B):
                for h in range(H):
                    nc.scalar.dma_start(out=g_raw[:, b, h, :, :], in_=gains[b, h].rearrange("(t p) j -> p t j", p=P))

            w_grouped = setup.tile([P, 2, 3 * P, 2], F32, name="w_grouped", align_bytes=64)
            for f in range(3):
                w_tr = ps_tr.tile([P, 4, P], F32, name="w_tr", tag="tr")
                words = w_sb[:, f, :].bitcast(F32)
                for j in range(4):
                    nc.tensor.transpose(out=w_tr[:, j, :], in_=words[:, j * P:(j + 1) * P], identity=ident[:])
                nc.vector.tensor_copy(out=w_grouped[:, :, f * P:(f + 1) * P, :],
                                      in_=w_tr[:].rearrange("p (g u) r -> p g r u", u=2))
            for g in range(2):
                for f in range(3):
                    nc.vector.quantize_mx(
                        out=w_codes[:, g, f * P:(f + 1) * P].bitcast(FP8X4),
                        scales=w_scales[:, g, f * P:(f + 1) * P],
                        in_=w_grouped[:, g, f * P:(f + 1) * P, :].rearrange("p r u -> p (r u)").bitcast(BF16))

            b_rows32 = setup.tile([P, P], F32, name="b_rows32")
            nc.vector.tensor_copy(out=b_rows32[:], in_=b_rows[:])
            b_tr = ps_tr.tile([P, 4, P], F32, name="b_tr", tag="tr")
            nc.tensor.transpose(out=b_tr[:, 0, :], in_=b_rows32[:], identity=ident[:])
            nc.vector.tensor_copy(out=bias_col[:, 0:3], in_=b_tr[:, 0, 0:3])

            nc.vector.memset(pb_bc[:], 0.0)
            nc.vector.tensor_copy(out=pb_bc[:, :, 1:NTAP].rearrange("p h (t j) -> p h t j", t=4),
                                  in_=pb_raw[:].rearrange("p (j t h) -> p h t j", t=4, h=H))

            ib = setup.tile([P, H], F32, name="ib")
            nc.vector.tensor_copy(out=ib[:], in_=ib_raw[:])
            ib_e = setup.tile([P, H], F32, name="ib_e")
            nc.scalar.activation(out=ib_e[:], in_=ib[:], func=ACTF.Abs)
            nc.scalar.activation(out=ib_e[:], in_=ib_e[:], func=ACTF.Exp, scale=-1.0)
            nc.vector.tensor_scalar_add(out=ib_e[:], in0=ib_e[:], scalar1=1.0)
            nc.scalar.activation(out=ib_e[:], in_=ib_e[:], func=ACTF.Ln)
            nc.vector.scalar_tensor_tensor(out=bypass[:], in0=ib[:], scalar=0.0, in1=ib_e[:],
                                           op0=ALU.max, op1=ALU.add)

        x_pool = ctx.enter_context(tc.tile_pool(name="x_pool", bufs=2))
        grouped_pool = ctx.enter_context(tc.tile_pool(name="grouped_pool", bufs=2))
        code_pool = ctx.enter_context(tc.tile_pool(name="code_pool", bufs=2))
        kf_pool = ctx.enter_context(tc.tile_pool(name="kf_pool", bufs=3))
        vf_pool = ctx.enter_context(tc.tile_pool(name="vf_pool", bufs=3))
        q_pool = ctx.enter_context(tc.tile_pool(name="q_pool", bufs=3))
        prod_pool = ctx.enter_context(tc.tile_pool(name="prod_pool", bufs=3))
        score_pool = ctx.enter_context(tc.tile_pool(name="score_pool", bufs=3))
        tap_pool = ctx.enter_context(tc.tile_pool(name="tap_pool", bufs=3))
        band_pool = ctx.enter_context(tc.tile_pool(name="band_pool", bufs=2))
        out_pool = ctx.enter_context(tc.tile_pool(name="out_pool", bufs=2))

        x_of, grouped_of, code_of = {}, {}, {}
        kf_of, vf_of, q_of = {}, {}, {}
        score_of, weight_of, skewed_of, band_of, o_of = {}, {}, {}, {}, {}
        scratch = out.rearrange("b n e -> (b n e)")

        def feature_major(c):
            if c not in kf_of:
                kf_of[c] = kf_pool.tile([P, KWIN + CH], F32, name="kf")
                vf_of[c] = vf_pool.tile([P, VWIN + CH], F32, name="vf")
            return kf_of[c], vf_of[c]

        def load_x(c):
            b, cc = divmod(c, NCC)
            x_of[c] = x_pool.tile([P, TPC, D], BF16, name="x_sb")
            nc.sync.dma_start(out=x_of[c][:],
                              in_=x[b, cc * CH:(cc + 1) * CH, :].rearrange("(t p) k -> p t k", p=P))

        def transpose_x(c, tl):
            if tl == 0:
                grouped_of[c] = grouped_pool.tile([P, 2, CH, 2], F32, name="grouped", align_bytes=64)
            x_tr = ps_tr.tile([P, 4, P], F32, name="x_tr", tag="tr")
            words = x_of[c][:, tl, :].bitcast(F32)
            for j in range(4):
                nc.tensor.transpose(out=x_tr[:, j, :], in_=words[:, j * P:(j + 1) * P], identity=ident[:])
            nc.scalar.copy(out=grouped_of[c][:, :, tl * P:(tl + 1) * P, :],
                           in_=x_tr[:].rearrange("p (g u) r -> p g r u", u=2))

        def quantise_x(c):
            codes = code_pool.tile([P, 2, CH], U32, name="codes", align_bytes=64)
            scales = code_pool.tile([P, 2, CH], U8, name="scales", align_bytes=64)
            for g in range(2):
                nc.vector.quantize_mx(
                    out=codes[:, g, :].bitcast(FP8X4), scales=scales[:, g, :],
                    in_=grouped_of[c][:, g, :, :].rearrange("p r u -> p (r u)").bitcast(BF16))
            code_of[c] = (codes, scales)

        def project(c, f):
            codes, scales = code_of[c]
            acc = ps_mx.tile([P, CH], F32, name="acc", tag="mx")
            for g in range(2):
                nc.tensor.matmul_mx(out=acc[:], lhsT=w_codes[:, g, f * P:(f + 1) * P].bitcast(FP8X4),
                                    lhsT_scale=w_scales[:, g, f * P:(f + 1) * P],
                                    rhs=codes[:, g, :].bitcast(FP8X4), rhs_scale=scales[:, g, :],
                                    start=(g == 0), stop=(g == 1))
            return acc

        def add_bias(dst, acc, f):
            nc.scalar.activation(out=dst, in_=acc, func=ACTF.Identity, bias=bias_col[:, f:f + 1], scale=1.0)

        def project_kv(c):
            cc = c % NCC
            for f, win in ((1, KWIN), (2, VWIN)):
                dst = feature_major(c)[f - 1]
                if cc == 0:
                    nc.vector.memset(dst[:, 0:win], 0.0)
                acc = project(c, f)
                add_bias(dst[:, win:win + CH], acc[:], f)
                if cc + 1 < NCC:
                    add_bias(feature_major(c + 1)[f - 1][:, 0:win], acc[:, CH - win:CH], f)

        def token_major(src, first, dst):
            tr = ps_tr.tile([P, TPC, P], F32, name="tok_tr", tag="tr")
            for tl in range(TPC):
                nc.tensor.transpose(out=tr[:, tl, :], in_=src[:, first + tl * P:first + (tl + 1) * P],
                                    identity=ident[:])
            nc.scalar.copy(out=dst, in_=tr[:])

        def project_q(c):
            q_f = q_pool.tile([P, CH], F32, name="q_f")
            add_bias(q_f[:], project(c, 0)[:], 0)
            q_of[c] = q_pool.tile([P, TPC, E], F32, name="q_tok")
            token_major(q_f, 0, q_of[c][:])

        def turn_kv(c):
            cc = c % NCC
            g0 = c * TPC
            token_major(kf_of[c], KWIN, k_tok[:, cc * TPC:(cc + 1) * TPC, :])
            token_major(vf_of[c], VWIN, v_tok[:, g0 % VRING:g0 % VRING + TPC, :])
            token_major(vf_of[c], 0, v_half[:, g0 % BRING:g0 % BRING + TPC, :])

        def scores(c, tl):
            cc = c % NCC
            if tl == 0:
                s_all = score_pool.tile([P, H, TPC, NOFF], F32, name="s_all")
                s_few = score_pool.tile([P, H, TPC, NFEW], F32, name="s_few")
                score_of[c] = (s_all, s_few)
                if n_valid(cc * TPC) < NOFF:
                    nc.vector.memset(s_all[:], 0.0)
            s_all, s_few = score_of[c]
            t = cc * TPC + tl
            nv = n_valid(t)
            q_t = q_of[c][:, tl, :]
            prod = prod_pool.tile([P, NOFF, E], F32, name="prod")
            for places in cut_groups(nv):
                cut = ps_cut.tile([P, 4, P], F32, name="cut", tag="cut")
                for i, s in enumerate(places):
                    first = KWIN + tl * P - OFFS[s]
                    nc.tensor.transpose(out=cut[:, i, :], in_=kf_of[c][:, first:first + P], identity=ident[:])
                for i0, s0, ln in runs_of(places):
                    nc.vector.tensor_tensor(out=prod[:, s0:s0 + ln, :], in0=cut[:, i0:i0 + ln, :],
                                            in1=q_t.unsqueeze(1).to_broadcast([P, ln, E]), op=ALU.mult)
            for s in range(nv):
                if OFFS[s] % P == 0:
                    nc.vector.tensor_tensor(out=prod[:, s, :], in0=k_tok[:, t - OFFS[s] // P, :], in1=q_t,
                                            op=ALU.mult)
            for s in range(NFEW):
                for h in range(H):
                    nc.scalar.activation(out=spare[:], in_=prod[:, s, h * HD:(h + 1) * HD], func=ACTF.Copy,
                                         accum_out=s_few[:, h, tl, s:s + 1])
            nc.vector.tensor_reduce(out=s_all[:, :, tl, NFEW:nv].rearrange("p h s -> p s h"),
                                    in_=prod[:, NFEW:nv, :].rearrange("p s (h d) -> p s h d", h=H),
                                    axis=AX.X, op=ALU.add)

        def weights(c):
            b, cc = divmod(c, NCC)
            s_all, s_few = score_of[c]
            shape = [P, H, TPC, NTAP]
            nf = (NFEW - 2) // 2
            few = s_few[:, :, :, 2:NFEW].rearrange("p h t (i two) -> p h t i two", two=2)
            pairs = s_all[:, :, :, NFEW:NOFF].rearrange("p h t (i two) -> p h t i two", two=2)
            u = tap_pool.tile(shape, F32, name="u")
            nc.scalar.copy(out=u[:, :, :, 0:12], in_=s_few[:, :, :, 0:1].to_broadcast([P, H, TPC, 12]))
            nc.scalar.copy(out=u[:, :, :, 12:13], in_=s_few[:, :, :, 1:2])
            nc.scalar.copy(out=u[:, :, :, 13:13 + nf], in_=few[:, :, :, :, 0])
            nc.scalar.copy(out=u[:, :, :, 13 + nf:23], in_=pairs[:, :, :, 0:10 - nf, 0])
            nc.scalar.copy(out=u[:, :, :, 23:23 + nf], in_=few[:, :, :, :, 0])
            nc.scalar.copy(out=u[:, :, :, 23 + nf:34], in_=pairs[:, :, :, 0:11 - nf, 0])
            nc.scalar.copy(out=u[:, :, :, 34:34 + nf], in_=few[:, :, :, :, 1])
            nc.scalar.copy(out=u[:, :, :, 34 + nf:45], in_=pairs[:, :, :, 0:11 - nf, 1])
            nc.vector.tensor_tensor(out=u[:], in0=u[:], in1=pb_bc[:].unsqueeze(2).to_broadcast(shape), op=ALU.add)
            f = tap_pool.tile(shape, F32, name="f")
            nc.scalar.activation(out=f[:], in_=u[:], func=ACTF.Exp)
            nc.scalar.activation(out=u[:], in_=u[:], func=ACTF.Relu)
            nc.vector.scalar_tensor_tensor(out=f[:].rearrange("p h t k -> p (h t k)"),
                                           in0=f[:].rearrange("p h t k -> p (h t k)"), scalar=1.0,
                                           in1=u[:].rearrange("p h t k -> p (h t k)"), op0=ALU.min, op1=ALU.add)
            gain = tap_pool.tile(shape, F32, name="gain")
            for tau in range(4):
                nc.scalar.activation(out=gain[:, :, :, 1 + NS * tau:1 + NS * (tau + 1)],
                                     in_=g_raw[:, b, :, cc * TPC:(cc + 1) * TPC, :], func=ACTF.Copy, scale=D4[tau])
            nc.scalar.copy(out=gain[:, :, :, 0:1],
                           in_=bypass[:].unsqueeze(2).unsqueeze(3).to_broadcast([P, H, TPC, 1]))
            w_tap = tap_pool.tile(shape, F32, name="w_tap")
            nc.vector.tensor_tensor(out=w_tap[:], in0=f[:], in1=gain[:], op=ALU.mult)
            z = tap_pool.tile([P, H, TPC], F32, name="z")
            rz = tap_pool.tile([P, H, TPC], F32, name="rz")
            nc.vector.tensor_reduce(out=z[:], in_=w_tap[:], axis=AX.X, op=ALU.add)
            nc.vector.tensor_reduce(out=rz[:], in_=w_tap[:, :, :, 34:45], axis=AX.X, op=ALU.add)
            nc.vector.scalar_tensor_tensor(out=z[:], in0=rz[:], scalar=-2.0, in1=z[:], op0=ALU.mult, op1=ALU.add)
            nc.vector.tensor_scalar_add(out=z[:], in0=z[:], scalar1=1e-6)
            nc.vector.reciprocal(out=rz[:], in_=z[:])
            w_zero = tap_pool.tile([P, H, TPC], F32, name="w_zero")
            nc.vector.tensor_reduce(out=w_zero[:], in_=w_tap[:, :, :, 0:12], axis=AX.X, op=ALU.add)
            w_pow = tap_pool.tile([P, H, TPC, 10], F32, name="w_pow")
            nc.vector.tensor_tensor(out=w_pow[:], in0=w_tap[:, :, :, 13:23], in1=w_tap[:, :, :, 23:33], op=ALU.add)

            def of_place(s):
                if s == 0:
                    return w_zero[:]
                if s == 1:
                    return w_tap[:, :, :, 12]
                if s % 2 == 1:
                    return w_tap[:, :, :, 34 + (s - 3) // 2]
                if s == NOFF - 2:
                    return w_tap[:, :, :, 33]
                return w_pow[:, :, :, s // 2 - 1]

            weight_of[c] = (of_place, rz)

        def skew(c):
            of_place = weight_of[c][0]
            for s in range(NEAR):
                nc.scalar.copy(out=rows[:, :, :, P - OFFS[s]], in_=of_place(s))
            for h in range(H):
                area = scratch[SCR0 + h * TPC * UNIT:SCR0 + (h + 1) * TPC * UNIT]
                nc.sync.dma_start(out=area.rearrange("(t p w) -> p t w", t=TPC, p=P), in_=rows[:, h, :, :])
                skewed_of[(c, h)] = band_pool.tile([P, TPC, 2 * P], F32, name="skewed")
                nc.sync.dma_start(out=skewed_of[(c, h)][:],
                                  in_=area.rearrange("(t r) -> t r", t=TPC)[:, 0:2 * P * P]
                                  .rearrange("t (p m) -> p t m", p=P))

        def band(c, h):
            band_of[(c, h)] = band_pool.tile([P, 2 * TPC, P], F32, name="band")
            for half in range(2):
                tr = ps_tr.tile([P, 4, P], F32, name="band_tr", tag="tr")
                for i in range(4):
                    tl, kb = divmod(4 * half + i, 2)
                    nc.tensor.transpose(out=tr[:, i, :], in_=skewed_of[(c, h)][:, tl, kb * P:(kb + 1) * P],
                                        identity=ident[:])
                nc.scalar.copy(out=band_of[(c, h)][:, 4 * half:4 * half + 4, :], in_=tr[:])

        def values(c, h):
            b, cc = divmod(c, NCC)
            of_place, rz = weight_of[c]
            hs = slice(h * HD, (h + 1) * HD)
            if h == 0:
                if c >= HOLD0:
                    o_of[c] = held[:, (c - HOLD0) * TPC:(c - HOLD0 + 1) * TPC, :]
                else:
                    o_of[c] = out_pool.tile([P, TPC, E], F32, name="o_sb")
            o_sb = o_of[c]
            near = ps_near.tile([P, TPC, HD], F32, name="near")
            for tl in range(TPC):
                blocks = [kb for kb in range(2) if cc * TPC + tl - 1 + kb >= 0]
                for kb in blocks:
                    nc.tensor.matmul(out=near[:, tl, :], lhsT=band_of[(c, h)][:, 2 * tl + kb, :],
                                     rhs=v_tok[:, (c * TPC + tl - 1 + kb) % VRING, hs],
                                     start=(kb == blocks[0]), stop=(kb == 1))
            total = [near[:, tl, :] for tl in range(TPC)]
            for s in range(NEAR, NOFF):
                for tl in range(TPC):
                    g = c * TPC + tl
                    if s < n_valid(cc * TPC + tl):
                        if OFFS[s] % P == 0:
                            shifted = v_tok[:, (g - OFFS[s] // P) % VRING, hs]
                        else:
                            shifted = v_half[:, (g - 1) % BRING, hs]
                        nc.vector.scalar_tensor_tensor(out=o_sb[:, tl, hs], in0=shifted,
                                                       scalar=of_place(s)[:, h, tl:tl + 1], in1=total[tl],
                                                       op0=ALU.mult, op1=ALU.add)
                        total[tl] = o_sb[:, tl, hs]
            for tl in range(TPC):
                nc.scalar.activation(out=o_sb[:, tl, hs], in_=total[tl], func=ACTF.Copy, scale=rz[:, h, tl:tl + 1])
            if h == H - 1 and c < HOLD0:
                nc.sync.dma_start(out=out[b, cc * CH:(cc + 1) * CH, :].rearrange("(t p) e -> p t e", p=P),
                                  in_=o_sb[:])

        def is_chunk(c):
            return 0 <= c < NCHUNK

        load_x(0)
        load_x(1)
        for c in range(-2, NCHUNK + 3):
            for tl in range(TPC):
                if tl == 0 and is_chunk(c + 3) and c + 3 >= 2:
                    load_x(c + 3)
                if is_chunk(c + 2):
                    transpose_x(c + 2, tl)
                if is_chunk(c + 1):
                    if tl == 0:
                        quantise_x(c + 1)
                    if tl == 1:
                        project_kv(c + 1)
                    if tl == 2:
                        project_q(c + 1)
                        turn_kv(c + 1)
                if is_chunk(c):
                    scores(c, tl)
                if tl == 1 and is_chunk(c - 1):
                    weights(c - 1)
                    skew(c - 1)
                if tl == 3 and is_chunk(c - 1):
                    band(c - 1, 0)
                if tl == 0 and is_chunk(c - 2):
                    band(c - 2, 1)
                    values(c - 2, 0)
                if tl == 1 and is_chunk(c - 2):
                    values(c - 2, 1)
        for c in range(HOLD0, NCHUNK):
            b, cc = divmod(c, NCC)
            nc.sync.dma_start(out=out[b, cc * CH:(cc + 1) * CH, :].rearrange("(t p) e -> p t e", p=P),
                              in_=held[:, (c - HOLD0) * TPC:(c - HOLD0 + 1) * TPC, :])
